import numpy as np
import ml_dtypes


def mxq(x, axis, fmt="e4m3"):
    dtype, down = {"e4m3": (ml_dtypes.float8_e4m3fn, 7), "e5m2": (ml_dtypes.float8_e5m2, 14)}[fmt]
    v = np.moveaxis(np.asarray(x, np.float32).astype(ml_dtypes.bfloat16).astype(np.float64), axis, -1)
    blocks = v.reshape(v.shape[:-1] + (-1, 32))
    amax = np.abs(blocks).max(-1, keepdims=True)
    byte = np.maximum(np.where(amax > 0, np.frexp(amax)[1] - 1 + 127, 0) - down, 1)
    scale = np.exp2(byte - 127.0)
    codes = (blocks / scale).astype(np.float32).astype(dtype).astype(np.float64)
    return np.moveaxis((codes * scale).reshape(v.shape), -1, axis)


WIDE = False


def mx_kscale(k):
    if not WIDE:
        return np.ones(k)
    levels = np.array([10, -10, 5, -5, 0])
    a = np.random.permutation(np.resize(levels, k // 512 * 4)).reshape(k // 512, 4)
    idx = np.arange(k)
    return np.exp2(a[idx // 512, idx % 128 // 32])


BF16 = ml_dtypes.bfloat16


def bf(x):
    return np.asarray(x, np.float32).astype(BF16)


def f64(x):
    return np.asarray(x).astype(np.float64)


N, D, O, KD = 8192, 256, 256, 8
BLK = 32


def cheby(t, kd):
    T = [np.ones_like(t), t]
    for _ in range(2, kd):
        T.append(2.0 * t * T[-1] - T[-2])
    return np.stack(T[:kd], axis=-1)


def setup_inputs():
    s = mx_kscale(D * KD)
    h = np.repeat(np.maximum(s.reshape(-1, BLK)[:, 0], 1.0), BLK // KD)
    x = np.random.standard_normal((N, D)) / h[None, :] ** 4
    c = np.random.standard_normal((O, D, KD)) / np.sqrt(D * KD)
    c[:, :, 1::2] *= h[None, :, None] ** 2
    c[:, :, 0::2] /= h[None, :, None] ** 2
    return {"x": bf(x),
            "cheby_coeffs": bf(c),
            "bias": bf(np.random.standard_normal((1, O)) * 0.2)}


def reference(x, cheby_coeffs, bias):
    xt = np.tanh(f64(x))
    T = cheby(xt, KD)
    Tf = T.reshape(N, D * KD)
    W = f64(cheby_coeffs).reshape(O, D * KD)
    y = mxq(Tf, 1, "e4m3") @ mxq(W, 1, "e4m3").T
    return y + f64(bias)

@@ -1,0 +1,172 @@
+from contextlib import ExitStack
+
+import concourse.bass as bass
+import concourse.mybir as mybir
+import concourse.tile as tile
+from concourse.masks import make_identity
+
+F32 = mybir.dt.float32
+BF16 = mybir.dt.bfloat16
+U32 = mybir.dt.uint32
+U8 = mybir.dt.uint8
+FP8X4 = mybir.dt.float8_e4m3fn_x4
+ALU = mybir.AluOpType
+ACTF = mybir.ActivationFunctionType
+
+P = 128
+N_TOK = 8192
+D_IN = 256
+KD = 8
+D_OUT = 256
+NT = N_TOK // P
+CH = 4
+NCH = NT // CH
+CT = CH * P
+FD = CT * 2
+FLOPS = 2 * N_TOK * D_OUT * D_IN * KD
+
+
+def tile_cfkanlayer_kernel(tc, x, cheby_coeffs, bias, out):
+    nc = tc.nc
+    x_v = x.rearrange("(p t) d -> p t d", t=NT)
+    out_v = out.rearrange("(p t) o -> p t o", t=NT)
+    with ExitStack() as ctx:
+        keep = ctx.enter_context(tc.tile_pool(name="keep", bufs=1))
+        work = ctx.enter_context(tc.tile_pool(name="work", bufs=2))
+        ps_x = ctx.enter_context(tc.psum_pool(name="ps_x", bufs=2))
+        ps_w = ctx.enter_context(tc.psum_pool(name="ps_w", bufs=2))
+        ps_o = ctx.enter_context(tc.psum_pool(name="ps_o", bufs=4))
+
+        x_sb = keep.tile([P, NT, D_IN], BF16)
+        cuts = [0, 4, 8, 16, 32, 64]
+        nc.sync.dma_start(out=x_sb[:, 0:4, :], in_=x_v[:, 0:4, :])
+        w_sb = keep.tile([P, 2, D_IN * KD], BF16)
+        nc.sync.dma_start(out=w_sb[:], in_=cheby_coeffs.rearrange("(h o) d k -> o h (d k)", h=2))
+        b_bf = keep.tile([P, D_OUT], BF16)
+        nc.sync.dma_start(out=b_bf[:], in_=bias.rearrange("a o -> (a o)").partition_broadcast(P))
+        for lo, hi in zip(cuts[1:-1], cuts[2:]):
+            nc.sync.dma_start(out=x_sb[:, lo:hi, :], in_=x_v[:, lo:hi, :])
+
+        ident = keep.tile([P, P], F32)
+        make_identity(nc, ident[:])
+        b_f32 = keep.tile([P, D_OUT], F32)
+        nc.vector.tensor_copy(out=b_f32[:], in_=b_bf[:])
+
+        g0 = []
+        for b in range(2):
+            g0_t = keep.tile([P, 2 * FD], BF16, name="g0_%d" % b, align_bytes=64)
+            nc.vector.memset(g0_t[:], 1.0)
+            g0.append(g0_t)
+
+        w_p = keep.tile([P, 2, KD, D_IN], BF16)
+        for h in range(2):
+            nc.vector.tensor_copy(
+                out=w_p[:, h].rearrange("o k (c a i) -> o k c a i", c=4, a=16, i=4),
+                in_=w_sb[:, h, :].rearrange("o (a c i k) -> o k c a i", a=16, c=4, i=4, k=KD),
+            )
+        w_g = keep.tile([P, 4, 2 * D_OUT], F32, align_bytes=64)
+        w_c = keep.tile([P, 4, D_OUT], U32, align_bytes=64)
+        w_s = keep.tile([P, 4, D_OUT], U8, align_bytes=64)
+        for m in range(4):
+            w_t = ps_w.tile([P, 2, D_OUT], F32)
+            for s in range(2):
+                for h in range(2):
+                    nc.tensor.transpose(
+                        w_t[:, s, h * P : (h + 1) * P], w_p[:, h, 2 * m + s, :].bitcast(F32), ident[:]
+                    )
+            nc.vector.tensor_copy(
+                out=w_g[:, m, :].rearrange("p (o s) -> p o s", s=2),
+                in_=w_t[:].rearrange("p s o -> p o s"),
+            )
+        nc.vector.quantize_mx(
+            out=w_c[:].rearrange("p m o -> p (m o)").bitcast(FP8X4),
+            scales=w_s[:].rearrange("p m o -> p (m o)"),
+            in_=w_g[:].rearrange("p m f -> p (m f)").bitcast(BF16),
+        )
+
+        for ci in range(NCH):
+            t0 = ci * CH
+            xp = work.tile([P, CH, D_IN], BF16)
+            nc.vector.tensor_copy(
+                out=xp[:].rearrange("p t (c a i) -> p t c a i", c=4, a=16, i=4),
+                in_=x_sb[:, t0 : t0 + CH, :].rearrange("p t (a c i) -> p t c a i", a=16, c=4, i=4),
+            )
+            x_t = ps_x.tile([P, CT], F32)
+            for tl in range(CH):
+                nc.tensor.transpose(x_t[:, tl * P : (tl + 1) * P], xp[:, tl, :].bitcast(F32), ident[:])
+
+            t = work.tile([P, FD], F32)
+            nc.scalar.activation(out=t[:], in_=x_t[:].bitcast(BF16), func=ACTF.Tanh)
+            u4 = work.tile([P, FD], F32)
+            nc.scalar.activation(out=u4[:], in_=t[:], func=ACTF.Square, scale=2.0)
+            v4 = work.tile([P, FD], F32)
+            nc.scalar.activation(out=v4[:], in_=u4[:], func=ACTF.Square, bias=-2.0)
+            q5 = work.tile([P, FD], F32)
+            nc.scalar.activation(out=q5[:], in_=u4[:], func=ACTF.Square, bias=-2.5)
+
+            g0_t = g0[ci % 2]
+            nc.vector.tensor_copy(
+                out=g0_t[:].rearrange("p (n s e) -> p n s e", s=2, e=2)[:, :, 1, :],
+                in_=t[:].rearrange("p (n e) -> p n e", e=2),
+            )
+            t3 = work.tile([P, FD], F32)
+            nc.vector.scalar_tensor_tensor(
+                out=t3[:], in0=u4[:], scalar=3.0, in1=t[:], op0=ALU.subtract, op1=ALU.mult
+            )
+            w6 = work.tile([P, FD], F32)
+            nc.scalar.activation(out=w6[:], in_=t3[:], func=ACTF.Square, scale=2.0)
+
+            pl1 = work.tile([P, 2, FD], BF16)
+            pl2 = work.tile([P, 2, FD], BF16)
+            pl3 = work.tile([P, 2, FD], BF16)
+            nc.scalar.activation(out=pl1[:, 0, :], in_=u4[:], func=ACTF.Identity, scale=0.5, bias=-1.0)
+            nc.scalar.copy(out=pl1[:, 1, :], in_=t3[:])
+            nc.scalar.activation(out=pl2[:, 0, :], in_=v4[:], func=ACTF.Identity, scale=0.5, bias=-1.0)
+            nc.vector.scalar_tensor_tensor(
+                out=pl2[:, 1, :], in0=q5[:], scalar=1.25, in1=t[:], op0=ALU.subtract, op1=ALU.mult
+            )
+            nc.scalar.activation(out=pl3[:, 0, :], in_=w6[:], func=ACTF.Identity, scale=0.5, bias=-1.0)
+            mm = work.tile([P, FD], F32)
+            nc.vector.scalar_tensor_tensor(
+                out=mm[:], in0=v4[:], scalar=2.0, in1=t3[:], op0=ALU.subtract, op1=ALU.mult
+            )
+            nc.vector.tensor_tensor(out=pl3[:, 1, :], in0=mm[:], in1=t[:], op=ALU.subtract)
+
+            codes = work.tile([P, 4, CT], U32, align_bytes=64)
+            scl = work.tile([P, 4, CT], U8, align_bytes=64)
+            grouped = [g0_t]
+            for m, pl in ((1, pl1), (2, pl2), (3, pl3)):
+                g_t = work.tile([P, 2 * FD], BF16, name="g%d" % m, align_bytes=64)
+                nc.vector.tensor_copy(
+                    out=g_t[:].rearrange("p (n s e) -> p n s e", s=2, e=2),
+                    in_=pl[:].rearrange("p s (n e) -> p n s e", e=2),
+                )
+                grouped.append(g_t)
+            for m in range(4):
+                nc.vector.quantize_mx(
+                    out=codes[:, m, :].bitcast(FP8X4), scales=scl[:, m, :], in_=grouped[m][:]
+                )
+
+            o_sb = work.tile([P, CH, D_OUT], F32)
+            for hp in range(CH // 2):
+                acc = ps_o.tile([P, 2, D_OUT], F32)
+                for j in range(2):
+                    tl = 2 * hp + j
+                    cols = slice(tl * P, (tl + 1) * P)
+                    for m in range(4):
+                        nc.tensor.matmul_mx(
+                            out=acc[:, j, :],
+                            lhsT=codes[:, m, cols].bitcast(FP8X4),
+                            lhsT_scale=scl[:, m, cols],
+                            rhs=w_c[:, m, :].bitcast(FP8X4),
+                            rhs_scale=w_s[:, m, :],
+                            start=(m == 0),
+                            stop=(m == 3),
+                        )
+                nc.vector.tensor_tensor(
+                    out=o_sb[:, 2 * hp : 2 * hp + 2, :],
+                    in0=acc[:],
+                    in1=b_f32[:].unsqueeze(1).to_broadcast([P, 2, D_OUT]),
+                    op=ALU.add,
+                )
+            nc.sync.dma_start(out=out_v[:, t0 : t0 + CH, :], in_=o_sb[:])

@@ -1,8 +1,6 @@
 from contextlib import ExitStack
 
-import concourse.bass as bass
 import concourse.mybir as mybir
-import concourse.tile as tile
 from concourse.masks import make_identity
 
 F32 = mybir.dt.float32
@@ -32,141 +30,190 @@ def tile_cfkanlayer_kernel(tc, x, cheby_coeffs, bias, out):
     out_v = out.rearrange("(p t) o -> p t o", t=NT)
     with ExitStack() as ctx:
         keep = ctx.enter_context(tc.tile_pool(name="keep", bufs=1))
-        work = ctx.enter_context(tc.tile_pool(name="work", bufs=2))
-        ps_x = ctx.enter_context(tc.psum_pool(name="ps_x", bufs=2))
-        ps_w = ctx.enter_context(tc.psum_pool(name="ps_w", bufs=2))
-        ps_o = ctx.enter_context(tc.psum_pool(name="ps_o", bufs=4))
+        ps = ctx.enter_context(tc.psum_pool(name="ps", bufs=1))
+        ctx.enter_context(tc.manual_schedule())
+
+        def ring(n, shape, dtype, name, pool=keep, align=None):
+            if align is None:
+                return [pool.tile(shape, dtype, name="%s_%d" % (name, b)) for b in range(n)]
+            return [pool.tile(shape, dtype, name="%s_%d" % (name, b), align_bytes=align) for b in range(n)]
 
         x_sb = keep.tile([P, NT, D_IN], BF16)
-        cuts = [0, 4, 8, 16, 32, 64]
-        nc.sync.dma_start(out=x_sb[:, 0:4, :], in_=x_v[:, 0:4, :])
         w_sb = keep.tile([P, 2, D_IN * KD], BF16)
-        nc.sync.dma_start(out=w_sb[:], in_=cheby_coeffs.rearrange("(h o) d k -> o h (d k)", h=2))
         b_bf = keep.tile([P, D_OUT], BF16)
+        nc.sync.dma_start(out=x_sb[:, 0:8, :], in_=x_v[:, 0:8, :])
+        nc.sync.dma_start(out=w_sb[:], in_=cheby_coeffs.rearrange("(h o) d k -> o h (d k)", h=2))
         nc.sync.dma_start(out=b_bf[:], in_=bias.rearrange("a o -> (a o)").partition_broadcast(P))
-        for lo, hi in zip(cuts[1:-1], cuts[2:]):
+        for lo, hi in ((8, 16), (16, 32), (32, 64)):
             nc.sync.dma_start(out=x_sb[:, lo:hi, :], in_=x_v[:, lo:hi, :])
 
         ident = keep.tile([P, P], F32)
         make_identity(nc, ident[:])
+
+        xp_r = ring(2, [P, CH, D_IN], BF16, "xp")
+        t_r = ring(2, [P, FD], F32, "t")
+        u4_r = ring(2, [P, FD], F32, "u4")
+        v4_r = ring(2, [P, FD], F32, "v4")
+        q5_r = ring(2, [P, FD], F32, "q5")
+        t3_r = ring(2, [P, FD], F32, "t3")
+        w6_r = ring(1, [P, FD], F32, "w6")
+        mm_r = ring(1, [P, FD], F32, "mm")
+        pl_r = [ring(2, [P, 2, FD], BF16, "pl%d" % m) for m in (1, 2, 3)]
+        g_r = ring(4, [P, 2 * FD], BF16, "g", align=64)
+        cod_r = ring(2, [P, 4, CT], U32, "cod", align=64)
+        scl_r = ring(2, [P, 4, CT], U8, "scl", align=64)
+        o_r = ring(2, [P, CH, D_OUT], F32, "o")
+        xt_r = ring(2, [P, CT], F32, "xt", pool=ps)
+        acc_r = ring(4, [P, 2, D_OUT], F32, "acc", pool=ps)
+        wt_r = ring(2, [P, 2, D_OUT], F32, "wt", pool=ps)
         b_f32 = keep.tile([P, D_OUT], F32)
-        nc.vector.tensor_copy(out=b_f32[:], in_=b_bf[:])
-
-        g0 = []
-        for b in range(2):
-            g0_t = keep.tile([P, 2 * FD], BF16, name="g0_%d" % b, align_bytes=64)
-            nc.vector.memset(g0_t[:], 1.0)
-            g0.append(g0_t)
-
         w_p = keep.tile([P, 2, KD, D_IN], BF16)
-        for h in range(2):
-            nc.vector.tensor_copy(
-                out=w_p[:, h].rearrange("o k (c a i) -> o k c a i", c=4, a=16, i=4),
-                in_=w_sb[:, h, :].rearrange("o (a c i k) -> o k c a i", a=16, c=4, i=4, k=KD),
-            )
         w_g = keep.tile([P, 4, 2 * D_OUT], F32, align_bytes=64)
         w_c = keep.tile([P, 4, D_OUT], U32, align_bytes=64)
         w_s = keep.tile([P, 4, D_OUT], U8, align_bytes=64)
-        for m in range(4):
-            w_t = ps_w.tile([P, 2, D_OUT], F32)
-            for s in range(2):
-                for h in range(2):
-                    nc.tensor.transpose(
-                        w_t[:, s, h * P : (h + 1) * P], w_p[:, h, 2 * m + s, :].bitcast(F32), ident[:]
-                    )
-            nc.vector.tensor_copy(
-                out=w_g[:, m, :].rearrange("p (o s) -> p o s", s=2),
-                in_=w_t[:].rearrange("p s o -> p o s"),
-            )
-        nc.vector.quantize_mx(
-            out=w_c[:].rearrange("p m o -> p (m o)").bitcast(FP8X4),
-            scales=w_s[:].rearrange("p m o -> p (m o)"),
-            in_=w_g[:].rearrange("p m f -> p (m f)").bitcast(BF16),
-        )
 
-        for ci in range(NCH):
-            t0 = ci * CH
-            xp = work.tile([P, CH, D_IN], BF16)
+        def ok(c):
+            return 0 <= c < NCH
+
+        def xperm(c):
             nc.vector.tensor_copy(
-                out=xp[:].rearrange("p t (c a i) -> p t c a i", c=4, a=16, i=4),
-                in_=x_sb[:, t0 : t0 + CH, :].rearrange("p t (a c i) -> p t c a i", a=16, c=4, i=4),
+                out=xp_r[c % 2][:].rearrange("p t (c a i) -> p t c a i", c=4, a=16, i=4),
+                in_=x_sb[:, c * CH : (c + 1) * CH, :].rearrange("p t (a c i) -> p t c a i", a=16, c=4, i=4),
             )
-            x_t = ps_x.tile([P, CT], F32)
+
+        def xtrans(c):
             for tl in range(CH):
-                nc.tensor.transpose(x_t[:, tl * P : (tl + 1) * P], xp[:, tl, :].bitcast(F32), ident[:])
+                nc.tensor.transpose(
+                    xt_r[c % 2][:, tl * P : (tl + 1) * P], xp_r[c % 2][:, tl, :].bitcast(F32), ident[:]
+                )
 
-            t = work.tile([P, FD], F32)
-            nc.scalar.activation(out=t[:], in_=x_t[:].bitcast(BF16), func=ACTF.Tanh)
-            u4 = work.tile([P, FD], F32)
-            nc.scalar.activation(out=u4[:], in_=t[:], func=ACTF.Square, scale=2.0)
-            v4 = work.tile([P, FD], F32)
-            nc.scalar.activation(out=v4[:], in_=u4[:], func=ACTF.Square, bias=-2.0)
-            q5 = work.tile([P, FD], F32)
-            nc.scalar.activation(out=q5[:], in_=u4[:], func=ACTF.Square, bias=-2.5)
+        def act(o, i, f, scale=1.0, bias_=0.0):
+            nc.scalar.activation(out=o, in_=i, func=f, scale=scale, bias=bias_)
 
-            g0_t = g0[ci % 2]
+        def stt(o, a, s, b):
+            nc.vector.scalar_tensor_tensor(out=o, in0=a, scalar=s, in1=b, op0=ALU.subtract, op1=ALU.mult)
+
+        def regroup(c, m):
             nc.vector.tensor_copy(
-                out=g0_t[:].rearrange("p (n s e) -> p n s e", s=2, e=2)[:, :, 1, :],
-                in_=t[:].rearrange("p (n e) -> p n e", e=2),
+                out=g_r[m][:].rearrange("p (n s e) -> p n s e", s=2, e=2),
+                in_=pl_r[m - 1][c % 2][:].rearrange("p s (n e) -> p n s e", e=2),
             )
-            t3 = work.tile([P, FD], F32)
-            nc.vector.scalar_tensor_tensor(
-                out=t3[:], in0=u4[:], scalar=3.0, in1=t[:], op0=ALU.subtract, op1=ALU.mult
-            )
-            w6 = work.tile([P, FD], F32)
-            nc.scalar.activation(out=w6[:], in_=t3[:], func=ACTF.Square, scale=2.0)
 
-            pl1 = work.tile([P, 2, FD], BF16)
-            pl2 = work.tile([P, 2, FD], BF16)
-            pl3 = work.tile([P, 2, FD], BF16)
-            nc.scalar.activation(out=pl1[:, 0, :], in_=u4[:], func=ACTF.Identity, scale=0.5, bias=-1.0)
-            nc.scalar.copy(out=pl1[:, 1, :], in_=t3[:])
-            nc.scalar.activation(out=pl2[:, 0, :], in_=v4[:], func=ACTF.Identity, scale=0.5, bias=-1.0)
-            nc.vector.scalar_tensor_tensor(
-                out=pl2[:, 1, :], in0=q5[:], scalar=1.25, in1=t[:], op0=ALU.subtract, op1=ALU.mult
+        def quant(c, m):
+            nc.vector.quantize_mx(
+                out=cod_r[c % 2][:, m, :].bitcast(FP8X4), scales=scl_r[c % 2][:, m, :], in_=g_r[m][:]
             )
-            nc.scalar.activation(out=pl3[:, 0, :], in_=w6[:], func=ACTF.Identity, scale=0.5, bias=-1.0)
-            mm = work.tile([P, FD], F32)
-            nc.vector.scalar_tensor_tensor(
-                out=mm[:], in0=v4[:], scalar=2.0, in1=t3[:], op0=ALU.subtract, op1=ALU.mult
-            )
-            nc.vector.tensor_tensor(out=pl3[:, 1, :], in0=mm[:], in1=t[:], op=ALU.subtract)
 
-            codes = work.tile([P, 4, CT], U32, align_bytes=64)
-            scl = work.tile([P, 4, CT], U8, align_bytes=64)
-            grouped = [g0_t]
-            for m, pl in ((1, pl1), (2, pl2), (3, pl3)):
-                g_t = work.tile([P, 2 * FD], BF16, name="g%d" % m, align_bytes=64)
-                nc.vector.tensor_copy(
-                    out=g_t[:].rearrange("p (n s e) -> p n s e", s=2, e=2),
-                    in_=pl[:].rearrange("p s (n e) -> p n s e", e=2),
-                )
-                grouped.append(g_t)
-            for m in range(4):
-                nc.vector.quantize_mx(
-                    out=codes[:, m, :].bitcast(FP8X4), scales=scl[:, m, :], in_=grouped[m][:]
-                )
-
-            o_sb = work.tile([P, CH, D_OUT], F32)
+        def mx(c):
             for hp in range(CH // 2):
-                acc = ps_o.tile([P, 2, D_OUT], F32)
+                acc = acc_r[2 * (c % 2) + hp]
                 for j in range(2):
-                    tl = 2 * hp + j
-                    cols = slice(tl * P, (tl + 1) * P)
+                    cols = slice((2 * hp + j) * P, (2 * hp + j + 1) * P)
                     for m in range(4):
                         nc.tensor.matmul_mx(
                             out=acc[:, j, :],
-                            lhsT=codes[:, m, cols].bitcast(FP8X4),
-                            lhsT_scale=scl[:, m, cols],
+                            lhsT=cod_r[c % 2][:, m, cols].bitcast(FP8X4),
+                            lhsT_scale=scl_r[c % 2][:, m, cols],
                             rhs=w_c[:, m, :].bitcast(FP8X4),
                             rhs_scale=w_s[:, m, :],
                             start=(m == 0),
                             stop=(m == 3),
                         )
-                nc.vector.tensor_tensor(
-                    out=o_sb[:, 2 * hp : 2 * hp + 2, :],
-                    in0=acc[:],
-                    in1=b_f32[:].unsqueeze(1).to_broadcast([P, 2, D_OUT]),
-                    op=ALU.add,
+
+        def outp(c, hp):
+            nc.vector.tensor_tensor(
+                out=o_r[c % 2][:, 2 * hp : 2 * hp + 2, :],
+                in0=acc_r[2 * (c % 2) + hp][:],
+                in1=b_f32[:].unsqueeze(1).to_broadcast([P, 2, D_OUT]),
+                op=ALU.add,
+            )
+
+        def w_perm():
+            for h in range(2):
+                nc.vector.tensor_copy(
+                    out=w_p[:, h].rearrange("o k (c a i) -> o k c a i", c=4, a=16, i=4),
+                    in_=w_sb[:, h, :].rearrange("o (a c i k) -> o k c a i", a=16, c=4, i=4, k=KD),
                 )
-            nc.sync.dma_start(out=out_v[:, t0 : t0 + CH, :], in_=o_sb[:])
+
+        def w_rest():
+            for m in range(4):
+                w_t = wt_r[m % 2]
+                for s in range(2):
+                    for h in range(2):
+                        nc.tensor.transpose(
+                            w_t[:, s, h * P : (h + 1) * P], w_p[:, h, 2 * m + s, :].bitcast(F32), ident[:]
+                        )
+                nc.vector.tensor_copy(
+                    out=w_g[:, m, :].rearrange("p (o s) -> p o s", s=2),
+                    in_=w_t[:].rearrange("p s o -> p o s"),
+                )
+            nc.vector.quantize_mx(
+                out=w_c[:].rearrange("p m o -> p (m o)").bitcast(FP8X4),
+                scales=w_s[:].rearrange("p m o -> p (m o)"),
+                in_=w_g[:].rearrange("p m f -> p (m f)").bitcast(BF16),
+            )
+            nc.vector.tensor_copy(out=b_f32[:], in_=b_bf[:])
+
+        xperm(0)
+        xtrans(0)
+        xperm(1)
+        xtrans(1)
+        nc.vector.memset(g_r[0][:], 1.0)
+        w_perm()
+
+        for i in range(NCH + 3):
+            a, b, c, d = i, i - 1, i - 2, i - 3
+            if ok(a):
+                act(t_r[a % 2][:], xt_r[a % 2][:].bitcast(BF16), ACTF.Tanh)
+            if ok(b):
+                act(w6_r[0][:], t3_r[b % 2][:], ACTF.Square, scale=2.0)
+            if ok(a):
+                act(u4_r[a % 2][:], t_r[a % 2][:], ACTF.Square, scale=2.0)
+            if ok(b):
+                nc.scalar.copy(out=pl_r[0][b % 2][:, 1, :], in_=t3_r[b % 2][:])
+            if ok(a):
+                act(v4_r[a % 2][:], u4_r[a % 2][:], ACTF.Square, bias_=-2.0)
+            if ok(b):
+                act(pl_r[0][b % 2][:, 0, :], u4_r[b % 2][:], ACTF.Identity, scale=0.5, bias_=-1.0)
+            if ok(a):
+                act(q5_r[a % 2][:], u4_r[a % 2][:], ACTF.Square, bias_=-2.5)
+            if ok(b):
+                act(pl_r[1][b % 2][:, 0, :], v4_r[b % 2][:], ACTF.Identity, scale=0.5, bias_=-1.0)
+                act(pl_r[2][b % 2][:, 0, :], w6_r[0][:], ACTF.Identity, scale=0.5, bias_=-1.0)
+            if ok(c):
+                regroup(c, 1)
+            if ok(b):
+                stt(pl_r[1][b % 2][:, 1, :], q5_r[b % 2][:], 1.25, t_r[b % 2][:])
+            if ok(c):
+                regroup(c, 2)
+            if ok(b):
+                stt(mm_r[0][:], v4_r[b % 2][:], 2.0, t3_r[b % 2][:])
+            if ok(c):
+                quant(c, 0)
+                regroup(c, 3)
+                quant(c, 1)
+            if ok(b):
+                nc.vector.tensor_tensor(
+                    out=pl_r[2][b % 2][:, 1, :], in0=mm_r[0][:], in1=t_r[b % 2][:], op=ALU.subtract
+                )
+            if ok(a + 1) and a + 1 >= 2:
+                xperm(a + 1)
+                xtrans(a + 1)
+            if ok(c):
+                quant(c, 2)
+            if ok(b):
+                nc.vector.tensor_copy(
+                    out=g_r[0][:].rearrange("p (n s e) -> p n s e", s=2, e=2)[:, :, 1, :],
+                    in_=t_r[b % 2][:].rearrange("p (n e) -> p n e", e=2),
+                )
+            if ok(c):
+                quant(c, 3)
+                mx(c)
+            if ok(a):
+                stt(t3_r[a % 2][:], u4_r[a % 2][:], 3.0, t_r[a % 2][:])
+            if i == 0:
+                w_rest()
+            if ok(d):
+                outp(d, 0)
+                outp(d, 1)
+                nc.sync.dma_start(out=out_v[:, d * CH : (d + 1) * CH, :], in_=o_r[d % 2][:])

@@ -60,6 +60,7 @@ def tile_cfkanlayer_kernel(tc, x, cheby_coeffs, bias, out):
         mm_r = ring(1, [P, FD], F32, "mm")
         pl_r = [ring(2, [P, 2, FD], BF16, "pl%d" % m) for m in (1, 2, 3)]
         g_r = ring(4, [P, 2 * FD], BF16, "g", align=64)
+        g0_r = [g_r[0], keep.tile([P, 2 * FD], BF16, name="g0b", align_bytes=64)]
         cod_r = ring(2, [P, 4, CT], U32, "cod", align=64)
         scl_r = ring(2, [P, 4, CT], U8, "scl", align=64)
         o_r = ring(2, [P, CH, D_OUT], F32, "o")
@@ -101,7 +102,9 @@ def tile_cfkanlayer_kernel(tc, x, cheby_coeffs, bias, out):
 
         def quant(c, m):
             nc.vector.quantize_mx(
-                out=cod_r[c % 2][:, m, :].bitcast(FP8X4), scales=scl_r[c % 2][:, m, :], in_=g_r[m][:]
+                out=cod_r[c % 2][:, m, :].bitcast(FP8X4),
+                scales=scl_r[c % 2][:, m, :],
+                in_=(g0_r[c % 2] if m == 0 else g_r[m])[:],
             )
 
         def mx(c):
@@ -143,7 +146,7 @@ def tile_cfkanlayer_kernel(tc, x, cheby_coeffs, bias, out):
                         nc.tensor.transpose(
                             w_t[:, s, h * P : (h + 1) * P], w_p[:, h, 2 * m + s, :].bitcast(F32), ident[:]
                         )
-                nc.vector.tensor_copy(
+                nc.scalar.copy(
                     out=w_g[:, m, :].rearrange("p (o s) -> p o s", s=2),
                     in_=w_t[:].rearrange("p s o -> p o s"),
                 )
@@ -152,13 +155,14 @@ def tile_cfkanlayer_kernel(tc, x, cheby_coeffs, bias, out):
                 scales=w_s[:].rearrange("p m o -> p (m o)"),
                 in_=w_g[:].rearrange("p m f -> p (m f)").bitcast(BF16),
             )
-            nc.vector.tensor_copy(out=b_f32[:], in_=b_bf[:])
+            nc.scalar.copy(out=b_f32[:], in_=b_bf[:])
 
         xperm(0)
         xtrans(0)
         xperm(1)
         xtrans(1)
-        nc.vector.memset(g_r[0][:], 1.0)
+        nc.vector.memset(g0_r[0][:], 1.0)
+        nc.vector.memset(g0_r[1][:], 1.0)
         w_perm()
 
         for i in range(NCH + 3):
@@ -170,7 +174,10 @@ def tile_cfkanlayer_kernel(tc, x, cheby_coeffs, bias, out):
             if ok(a):
                 act(u4_r[a % 2][:], t_r[a % 2][:], ACTF.Square, scale=2.0)
             if ok(b):
-                nc.scalar.copy(out=pl_r[0][b % 2][:, 1, :], in_=t3_r[b % 2][:])
+                nc.scalar.copy(
+                    out=g0_r[b % 2][:].rearrange("p (n s e) -> p n s e", s=2, e=2)[:, :, 1, :],
+                    in_=t_r[b % 2][:].rearrange("p (n e) -> p n e", e=2),
+                )
             if ok(a):
                 act(v4_r[a % 2][:], u4_r[a % 2][:], ACTF.Square, bias_=-2.0)
             if ok(b):
@@ -201,16 +208,14 @@ def tile_cfkanlayer_kernel(tc, x, cheby_coeffs, bias, out):
                 xtrans(a + 1)
             if ok(c):
                 quant(c, 2)
-            if ok(b):
-                nc.vector.tensor_copy(
-                    out=g_r[0][:].rearrange("p (n s e) -> p n s e", s=2, e=2)[:, :, 1, :],
-                    in_=t_r[b % 2][:].rearrange("p (n e) -> p n e", e=2),
-                )
             if ok(c):
                 quant(c, 3)
                 mx(c)
             if ok(a):
                 stt(t3_r[a % 2][:], u4_r[a % 2][:], 3.0, t_r[a % 2][:])
+                nc.gpsimd.tensor_scalar(
+                    out=pl_r[0][a % 2][:, 1, :], in0=t3_r[a % 2][:], scalar1=1.0, scalar2=0.0, op0=ALU.mult, op1=ALU.add
+                )
             if i == 0:
                 w_rest()
             if ok(d):

@@ -7,6 +7,7 @@ F32 = mybir.dt.float32
 BF16 = mybir.dt.bfloat16
 U32 = mybir.dt.uint32
 U8 = mybir.dt.uint8
+I32 = mybir.dt.int32
 FP8X4 = mybir.dt.float8_e4m3fn_x4
 ALU = mybir.AluOpType
 ACTF = mybir.ActivationFunctionType
@@ -96,8 +97,8 @@ def tile_cfkanlayer_kernel(tc, x, cheby_coeffs, bias, out):
 
         def regroup(c, m):
             nc.vector.tensor_copy(
-                out=g_r[m][:].rearrange("p (n s e) -> p n s e", s=2, e=2),
-                in_=pl_r[m - 1][c % 2][:].rearrange("p s (n e) -> p n s e", e=2),
+                out=g_r[m][:].bitcast(I32).rearrange("p (n s) -> p n s", s=2),
+                in_=pl_r[m - 1][c % 2][:].bitcast(I32).rearrange("p s n -> p n s"),
             )
 
         def quant(c, m):

@@ -7,7 +7,6 @@ F32 = mybir.dt.float32
 BF16 = mybir.dt.bfloat16
 U32 = mybir.dt.uint32
 U8 = mybir.dt.uint8
-I32 = mybir.dt.int32
 FP8X4 = mybir.dt.float8_e4m3fn_x4
 ALU = mybir.AluOpType
 ACTF = mybir.ActivationFunctionType
@@ -22,6 +21,7 @@ CH = 4
 NCH = NT // CH
 CT = CH * P
 FD = CT * 2
+HF = FD // 2
 FLOPS = 2 * N_TOK * D_OUT * D_IN * KD
 
 
@@ -97,8 +97,8 @@ def tile_cfkanlayer_kernel(tc, x, cheby_coeffs, bias, out):
 
         def regroup(c, m):
             nc.vector.tensor_copy(
-                out=g_r[m][:].bitcast(I32).rearrange("p (n s) -> p n s", s=2),
-                in_=pl_r[m - 1][c % 2][:].bitcast(I32).rearrange("p s n -> p n s"),
+                out=g_r[m][:].rearrange("p (n s e) -> p n s e", s=2, e=2),
+                in_=pl_r[m - 1][c % 2][:].rearrange("p s (n e) -> p n s e", e=2),
             )
 
         def quant(c, m):
@@ -198,6 +198,9 @@ def tile_cfkanlayer_kernel(tc, x, cheby_coeffs, bias, out):
                 stt(mm_r[0][:], v4_r[b % 2][:], 2.0, t3_r[b % 2][:])
             if ok(c):
                 quant(c, 0)
+            if ok(b):
+                nc.vector.tensor_copy(out=pl_r[0][b % 2][:, 1, HF:FD], in_=t3_r[b % 2][:, HF:FD])
+            if ok(c):
                 regroup(c, 3)
                 quant(c, 1)
             if ok(b):
@@ -215,7 +218,12 @@ def tile_cfkanlayer_kernel(tc, x, cheby_coeffs, bias, out):
             if ok(a):
                 stt(t3_r[a % 2][:], u4_r[a % 2][:], 3.0, t_r[a % 2][:])
                 nc.gpsimd.tensor_scalar(
-                    out=pl_r[0][a % 2][:, 1, :], in0=t3_r[a % 2][:], scalar1=1.0, scalar2=0.0, op0=ALU.mult, op1=ALU.add
+                    out=pl_r[0][a % 2][:, 1, 0:HF],
+                    in0=t3_r[a % 2][:, 0:HF],
+                    scalar1=1.0,
+                    scalar2=0.0,
+                    op0=ALU.mult,
+                    op1=ALU.add,
                 )
             if i == 0:
                 w_rest()

@@ -21,7 +21,7 @@ CH = 4
 NCH = NT // CH
 CT = CH * P
 FD = CT * 2
-HF = FD // 2
+NV = 192
 FLOPS = 2 * N_TOK * D_OUT * D_IN * KD
 
 
@@ -176,8 +176,8 @@ def tile_cfkanlayer_kernel(tc, x, cheby_coeffs, bias, out):
                 act(u4_r[a % 2][:], t_r[a % 2][:], ACTF.Square, scale=2.0)
             if ok(b):
                 nc.scalar.copy(
-                    out=g0_r[b % 2][:].rearrange("p (n s e) -> p n s e", s=2, e=2)[:, :, 1, :],
-                    in_=t_r[b % 2][:].rearrange("p (n e) -> p n e", e=2),
+                    out=g0_r[b % 2][:].rearrange("p (n s e) -> p n s e", s=2, e=2)[:, NV:CT, 1, :],
+                    in_=t_r[b % 2][:].rearrange("p (n e) -> p n e", e=2)[:, NV:CT, :],
                 )
             if ok(a):
                 act(v4_r[a % 2][:], u4_r[a % 2][:], ACTF.Square, bias_=-2.0)
@@ -198,9 +198,6 @@ def tile_cfkanlayer_kernel(tc, x, cheby_coeffs, bias, out):
                 stt(mm_r[0][:], v4_r[b % 2][:], 2.0, t3_r[b % 2][:])
             if ok(c):
                 quant(c, 0)
-            if ok(b):
-                nc.vector.tensor_copy(out=pl_r[0][b % 2][:, 1, HF:FD], in_=t3_r[b % 2][:, HF:FD])
-            if ok(c):
                 regroup(c, 3)
                 quant(c, 1)
             if ok(b):
@@ -212,18 +209,18 @@ def tile_cfkanlayer_kernel(tc, x, cheby_coeffs, bias, out):
                 xtrans(a + 1)
             if ok(c):
                 quant(c, 2)
+            if ok(b):
+                nc.vector.tensor_copy(
+                    out=g0_r[b % 2][:].rearrange("p (n s e) -> p n s e", s=2, e=2)[:, 0:NV, 1, :],
+                    in_=t_r[b % 2][:].rearrange("p (n e) -> p n e", e=2)[:, 0:NV, :],
+                )
             if ok(c):
                 quant(c, 3)
                 mx(c)
             if ok(a):
                 stt(t3_r[a % 2][:], u4_r[a % 2][:], 3.0, t_r[a % 2][:])
                 nc.gpsimd.tensor_scalar(
-                    out=pl_r[0][a % 2][:, 1, 0:HF],
-                    in0=t3_r[a % 2][:, 0:HF],
-                    scalar1=1.0,
-                    scalar2=0.0,
-                    op0=ALU.mult,
-                    op1=ALU.add,
+                    out=pl_r[0][a % 2][:, 1, :], in0=t3_r[a % 2][:], scalar1=1.0, scalar2=0.0, op0=ALU.mult, op1=ALU.add
                 )
             if i == 0:
                 w_rest()

@@ -21,7 +21,6 @@ CH = 4
 NCH = NT // CH
 CT = CH * P
 FD = CT * 2
-NV = 192
 FLOPS = 2 * N_TOK * D_OUT * D_IN * KD
 
 
@@ -53,15 +52,13 @@ def tile_cfkanlayer_kernel(tc, x, cheby_coeffs, bias, out):
 
         xp_r = ring(2, [P, CH, D_IN], BF16, "xp")
         t_r = ring(2, [P, FD], F32, "t")
-        u4_r = ring(2, [P, FD], F32, "u4")
-        v4_r = ring(2, [P, FD], F32, "v4")
+        sq_r = ring(2, [P, 3, FD], F32, "sq")
         q5_r = ring(2, [P, FD], F32, "q5")
         t3_r = ring(2, [P, FD], F32, "t3")
-        w6_r = ring(1, [P, FD], F32, "w6")
         mm_r = ring(1, [P, FD], F32, "mm")
-        pl_r = [ring(2, [P, 2, FD], BF16, "pl%d" % m) for m in (1, 2, 3)]
-        g_r = ring(4, [P, 2 * FD], BF16, "g", align=64)
-        g0_r = [g_r[0], keep.tile([P, 2 * FD], BF16, name="g0b", align_bytes=64)]
+        pl_r = ring(2, [P, 3, 2, FD], BF16, "pl")
+        g_t = keep.tile([P, 3, 2 * FD], BF16, align_bytes=64)
+        g0_r = ring(2, [P, 2 * FD], BF16, "g0", align=64)
         cod_r = ring(2, [P, 4, CT], U32, "cod", align=64)
         scl_r = ring(2, [P, 4, CT], U8, "scl", align=64)
         o_r = ring(2, [P, CH, D_OUT], F32, "o")
@@ -95,17 +92,17 @@ def tile_cfkanlayer_kernel(tc, x, cheby_coeffs, bias, out):
         def stt(o, a, s, b):
             nc.vector.scalar_tensor_tensor(out=o, in0=a, scalar=s, in1=b, op0=ALU.subtract, op1=ALU.mult)
 
-        def regroup(c, m):
+        def regroup(c):
             nc.vector.tensor_copy(
-                out=g_r[m][:].rearrange("p (n s e) -> p n s e", s=2, e=2),
-                in_=pl_r[m - 1][c % 2][:].rearrange("p s (n e) -> p n s e", e=2),
+                out=g_t[:].rearrange("p m (n s e) -> p m n s e", s=2, e=2),
+                in_=pl_r[c % 2][:].rearrange("p m s (n e) -> p m n s e", e=2),
             )
 
-        def quant(c, m):
+        def quant(c, m0, m1):
             nc.vector.quantize_mx(
-                out=cod_r[c % 2][:, m, :].bitcast(FP8X4),
-                scales=scl_r[c % 2][:, m, :],
-                in_=(g0_r[c % 2] if m == 0 else g_r[m])[:],
+                out=cod_r[c % 2][:, m0:m1, :].rearrange("p m n -> p (m n)").bitcast(FP8X4),
+                scales=scl_r[c % 2][:, m0:m1, :].rearrange("p m n -> p (m n)"),
+                in_=g0_r[c % 2][:] if m0 == 0 else g_t[:, m0 - 1 : m1 - 1, :].rearrange("p m f -> p (m f)"),
             )
 
         def mx(c):
@@ -171,56 +168,42 @@ def tile_cfkanlayer_kernel(tc, x, cheby_coeffs, bias, out):
             if ok(a):
                 act(t_r[a % 2][:], xt_r[a % 2][:].bitcast(BF16), ACTF.Tanh)
             if ok(b):
-                act(w6_r[0][:], t3_r[b % 2][:], ACTF.Square, scale=2.0)
+                act(sq_r[b % 2][:, 2, :], t3_r[b % 2][:], ACTF.Square, scale=2.0)
             if ok(a):
-                act(u4_r[a % 2][:], t_r[a % 2][:], ACTF.Square, scale=2.0)
+                act(sq_r[a % 2][:, 0, :], t_r[a % 2][:], ACTF.Square, scale=2.0)
             if ok(b):
                 nc.scalar.copy(
-                    out=g0_r[b % 2][:].rearrange("p (n s e) -> p n s e", s=2, e=2)[:, NV:CT, 1, :],
-                    in_=t_r[b % 2][:].rearrange("p (n e) -> p n e", e=2)[:, NV:CT, :],
+                    out=g0_r[b % 2][:].rearrange("p (n s e) -> p n s e", s=2, e=2)[:, :, 1, :],
+                    in_=t_r[b % 2][:].rearrange("p (n e) -> p n e", e=2),
                 )
             if ok(a):
-                act(v4_r[a % 2][:], u4_r[a % 2][:], ACTF.Square, bias_=-2.0)
+                act(sq_r[a % 2][:, 1, :], sq_r[a % 2][:, 0, :], ACTF.Square, bias_=-2.0)
+                act(q5_r[a % 2][:], sq_r[a % 2][:, 0, :], ACTF.Square, bias_=-2.5)
             if ok(b):
-                act(pl_r[0][b % 2][:, 0, :], u4_r[b % 2][:], ACTF.Identity, scale=0.5, bias_=-1.0)
-            if ok(a):
-                act(q5_r[a % 2][:], u4_r[a % 2][:], ACTF.Square, bias_=-2.5)
+                act(pl_r[b % 2][:, :, 0, :], sq_r[b % 2][:], ACTF.Identity, scale=0.5, bias_=-1.0)
             if ok(b):
-                act(pl_r[1][b % 2][:, 0, :], v4_r[b % 2][:], ACTF.Identity, scale=0.5, bias_=-1.0)
-                act(pl_r[2][b % 2][:, 0, :], w6_r[0][:], ACTF.Identity, scale=0.5, bias_=-1.0)
+                stt(pl_r[b % 2][:, 1, 1, :], q5_r[b % 2][:], 1.25, t_r[b % 2][:])
             if ok(c):
-                regroup(c, 1)
+                regroup(c)
             if ok(b):
-                stt(pl_r[1][b % 2][:, 1, :], q5_r[b % 2][:], 1.25, t_r[b % 2][:])
+                stt(mm_r[0][:], sq_r[b % 2][:, 1, :], 2.0, t3_r[b % 2][:])
             if ok(c):
-                regroup(c, 2)
-            if ok(b):
-                stt(mm_r[0][:], v4_r[b % 2][:], 2.0, t3_r[b % 2][:])
-            if ok(c):
-                quant(c, 0)
-                regroup(c, 3)
-                quant(c, 1)
+                quant(c, 0, 1)
+                quant(c, 1, 2)
             if ok(b):
                 nc.vector.tensor_tensor(
-                    out=pl_r[2][b % 2][:, 1, :], in0=mm_r[0][:], in1=t_r[b % 2][:], op=ALU.subtract
+                    out=pl_r[b % 2][:, 2, 1, :], in0=mm_r[0][:], in1=t_r[b % 2][:], op=ALU.subtract
                 )
+            if ok(c):
+                quant(c, 2, 4)
+                mx(c)
             if ok(a + 1) and a + 1 >= 2:
                 xperm(a + 1)
                 xtrans(a + 1)
-            if ok(c):
-                quant(c, 2)
-            if ok(b):
-                nc.vector.tensor_copy(
-                    out=g0_r[b % 2][:].rearrange("p (n s e) -> p n s e", s=2, e=2)[:, 0:NV, 1, :],
-                    in_=t_r[b % 2][:].rearrange("p (n e) -> p n e", e=2)[:, 0:NV, :],
-                )
-            if ok(c):
-                quant(c, 3)
-                mx(c)
             if ok(a):
-                stt(t3_r[a % 2][:], u4_r[a % 2][:], 3.0, t_r[a % 2][:])
+                stt(t3_r[a % 2][:], sq_r[a % 2][:, 0, :], 3.0, t_r[a % 2][:])
                 nc.gpsimd.tensor_scalar(
-                    out=pl_r[0][a % 2][:, 1, :], in0=t3_r[a % 2][:], scalar1=1.0, scalar2=0.0, op0=ALU.mult, op1=ALU.add
+                    out=pl_r[a % 2][:, 0, 1, :], in0=t3_r[a % 2][:], scalar1=1.0, scalar2=0.0, op0=ALU.mult, op1=ALU.add
                 )
             if i == 0:
                 w_rest()

@@ -92,10 +92,10 @@ def tile_cfkanlayer_kernel(tc, x, cheby_coeffs, bias, out):
         def stt(o, a, s, b):
             nc.vector.scalar_tensor_tensor(out=o, in0=a, scalar=s, in1=b, op0=ALU.subtract, op1=ALU.mult)
 
-        def regroup(c):
+        def regroup(c, m0, m1):
             nc.vector.tensor_copy(
-                out=g_t[:].rearrange("p m (n s e) -> p m n s e", s=2, e=2),
-                in_=pl_r[c % 2][:].rearrange("p m s (n e) -> p m n s e", e=2),
+                out=g_t[:, m0:m1, :].rearrange("p m (n s e) -> p m n s e", s=2, e=2),
+                in_=pl_r[c % 2][:, m0:m1].rearrange("p m s (n e) -> p m n s e", e=2),
             )
 
         def quant(c, m0, m1):
@@ -172,34 +172,36 @@ def tile_cfkanlayer_kernel(tc, x, cheby_coeffs, bias, out):
             if ok(a):
                 act(sq_r[a % 2][:, 0, :], t_r[a % 2][:], ACTF.Square, scale=2.0)
             if ok(b):
+                act(pl_r[b % 2][:, :, 0, :], sq_r[b % 2][:], ACTF.Identity, scale=0.5, bias_=-1.0)
+            if ok(a):
+                act(sq_r[a % 2][:, 1, :], sq_r[a % 2][:, 0, :], ACTF.Square, bias_=-2.0)
+            if ok(b):
                 nc.scalar.copy(
                     out=g0_r[b % 2][:].rearrange("p (n s e) -> p n s e", s=2, e=2)[:, :, 1, :],
                     in_=t_r[b % 2][:].rearrange("p (n e) -> p n e", e=2),
                 )
             if ok(a):
-                act(sq_r[a % 2][:, 1, :], sq_r[a % 2][:, 0, :], ACTF.Square, bias_=-2.0)
                 act(q5_r[a % 2][:], sq_r[a % 2][:, 0, :], ACTF.Square, bias_=-2.5)
-            if ok(b):
-                act(pl_r[b % 2][:, :, 0, :], sq_r[b % 2][:], ACTF.Identity, scale=0.5, bias_=-1.0)
-            if ok(b):
-                stt(pl_r[b % 2][:, 1, 1, :], q5_r[b % 2][:], 1.25, t_r[b % 2][:])
+            if ok(a + 1) and a + 1 >= 2:
+                xperm(a + 1)
+                xtrans(a + 1)
             if ok(c):
-                regroup(c)
+                regroup(c, 0, 2)
+                regroup(c, 2, 3)
             if ok(b):
                 stt(mm_r[0][:], sq_r[b % 2][:, 1, :], 2.0, t3_r[b % 2][:])
             if ok(c):
-                quant(c, 0, 1)
                 quant(c, 1, 2)
             if ok(b):
                 nc.vector.tensor_tensor(
                     out=pl_r[b % 2][:, 2, 1, :], in0=mm_r[0][:], in1=t_r[b % 2][:], op=ALU.subtract
                 )
             if ok(c):
+                quant(c, 0, 1)
                 quant(c, 2, 4)
                 mx(c)
-            if ok(a + 1) and a + 1 >= 2:
-                xperm(a + 1)
-                xtrans(a + 1)
+            if ok(b):
+                stt(pl_r[b % 2][:, 1, 1, :], q5_r[b % 2][:], 1.25, t_r[b % 2][:])
             if ok(a):
                 stt(t3_r[a % 2][:], sq_r[a % 2][:, 0, :], 3.0, t_r[a % 2][:])
                 nc.gpsimd.tensor_scalar(

@@ -21,6 +21,7 @@ CH = 4
 NCH = NT // CH
 CT = CH * P
 FD = CT * 2
+SRG = (1, 3)
 FLOPS = 2 * N_TOK * D_OUT * D_IN * KD
 
 
@@ -50,59 +51,89 @@ def tile_cfkanlayer_kernel(tc, x, cheby_coeffs, bias, out):
         ident = keep.tile([P, P], F32)
         make_identity(nc, ident[:])
 
-        xp_r = ring(2, [P, CH, D_IN], BF16, "xp")
-        t_r = ring(2, [P, FD], F32, "t")
-        sq_r = ring(2, [P, 3, FD], F32, "sq")
+        tn_r = ring(2, [P, CH, D_IN], F32, "tn")
+        z_r = ring(2, [P, FD], F32, "z")
+        v4_r = ring(2, [P, FD], F32, "v4")
+        w6_r = ring(2, [P, FD], F32, "w6")
         q5_r = ring(2, [P, FD], F32, "q5")
         t3_r = ring(2, [P, FD], F32, "t3")
         mm_r = ring(1, [P, FD], F32, "mm")
-        pl_r = ring(2, [P, 3, 2, FD], BF16, "pl")
-        g_t = keep.tile([P, 3, 2 * FD], BF16, align_bytes=64)
-        g0_r = ring(2, [P, 2 * FD], BF16, "g0", align=64)
+        pl_r = [ring(1 if m == 2 else 2, [P, 2, FD], BF16, "pl%d" % m) for m in range(1, 4)]
+        g_r = ring(2, [P, 4, 2 * FD], BF16, "g", align=64)
         cod_r = ring(2, [P, 4, CT], U32, "cod", align=64)
         scl_r = ring(2, [P, 4, CT], U8, "scl", align=64)
         o_r = ring(2, [P, CH, D_OUT], F32, "o")
-        xt_r = ring(2, [P, CT], F32, "xt", pool=ps)
+        tp_r = ring(2, [P, 2, 2, 2 * P], F32, "tp", pool=ps)
         acc_r = ring(4, [P, 2, D_OUT], F32, "acc", pool=ps)
-        wt_r = ring(2, [P, 2, D_OUT], F32, "wt", pool=ps)
         b_f32 = keep.tile([P, D_OUT], F32)
-        w_p = keep.tile([P, 2, KD, D_IN], BF16)
-        w_g = keep.tile([P, 4, 2 * D_OUT], F32, align_bytes=64)
+        w_p = keep.tile([P, 2, KD // 2, D_IN], F32)
+        w_g = keep.tile([P, 4, 4 * D_OUT], BF16, align_bytes=64)
         w_c = keep.tile([P, 4, D_OUT], U32, align_bytes=64)
         w_s = keep.tile([P, 4, D_OUT], U8, align_bytes=64)
 
         def ok(c):
             return 0 <= c < NCH
 
-        def xperm(c):
-            nc.vector.tensor_copy(
-                out=xp_r[c % 2][:].rearrange("p t (c a i) -> p t c a i", c=4, a=16, i=4),
-                in_=x_sb[:, c * CH : (c + 1) * CH, :].rearrange("p t (a c i) -> p t c a i", a=16, c=4, i=4),
-            )
-
-        def xtrans(c):
-            for tl in range(CH):
-                nc.tensor.transpose(
-                    xt_r[c % 2][:, tl * P : (tl + 1) * P], xp_r[c % 2][:, tl, :].bitcast(F32), ident[:]
-                )
-
         def act(o, i, f, scale=1.0, bias_=0.0):
             nc.scalar.activation(out=o, in_=i, func=f, scale=scale, bias=bias_)
+
+        def t_ps(c):
+            return tp_r[c % 2][:].rearrange("p g h n -> p (g h n)")
+
+        def half(ap, g):
+            return ap[:, g * (FD // 2) : (g + 1) * (FD // 2)]
+
+        def nh(ap):
+            return ap.rearrange("p (g h n) -> p g n h", g=2, h=2)
+
+        def gnh(ap):
+            return ap.rearrange("p (g n h) -> p g n h", g=2, h=2)
+
+        def tanh(c):
+            for tl in range(CH):
+                act(
+                    tn_r[c % 2][:, tl, :].rearrange("p (y b i) -> p y b i", y=8, b=8, i=4),
+                    x_sb[:, c * CH + tl, :].rearrange("p (b y i) -> p y b i", y=8, b=8, i=4),
+                    ACTF.Tanh,
+                )
+
+        def ttrans(c):
+            for tl in range(CH):
+                for h in range(2):
+                    nc.tensor.transpose(
+                        tp_r[c % 2][:, tl // 2, h, (tl % 2) * P : (tl % 2 + 1) * P],
+                        tn_r[c % 2][:, tl, h * P : (h + 1) * P],
+                        ident[:],
+                    )
 
         def stt(o, a, s, b):
             nc.vector.scalar_tensor_tensor(out=o, in0=a, scalar=s, in1=b, op0=ALU.subtract, op1=ALU.mult)
 
-        def regroup(c, m0, m1):
-            nc.vector.tensor_copy(
-                out=g_t[:, m0:m1, :].rearrange("p m (n s e) -> p m n s e", s=2, e=2),
-                in_=pl_r[c % 2][:, m0:m1].rearrange("p m s (n e) -> p m n s e", e=2),
-            )
+        def gaff(o, i, s, b):
+            nc.gpsimd.tensor_scalar(out=gnh(o), in0=nh(i), scalar1=s, scalar2=b, op0=ALU.mult, op1=ALU.add)
+
+        def pl(c, m, s):
+            return pl_r[m - 1][c % len(pl_r[m - 1])][:, s, :]
+
+        def regroup(c, m):
+            src = pl_r[m - 1][c % len(pl_r[m - 1])][:]
+            dst = g_r[c % 2][:, m, :]
+            if m in SRG:
+                nc.scalar.copy(
+                    out=dst.bitcast(F32).rearrange("p (n s) -> p n s", s=2),
+                    in_=src.bitcast(F32).rearrange("p s n -> p n s"),
+                )
+            else:
+                nc.vector.tensor_copy(
+                    out=dst.rearrange("p (n s e) -> p n s e", s=2, e=2),
+                    in_=src.rearrange("p s (n e) -> p n s e", e=2),
+                )
 
         def quant(c, m0, m1):
             nc.vector.quantize_mx(
                 out=cod_r[c % 2][:, m0:m1, :].rearrange("p m n -> p (m n)").bitcast(FP8X4),
                 scales=scl_r[c % 2][:, m0:m1, :].rearrange("p m n -> p (m n)"),
-                in_=g0_r[c % 2][:] if m0 == 0 else g_t[:, m0 - 1 : m1 - 1, :].rearrange("p m f -> p (m f)"),
+                in_=g_r[c % 2][:, m0:m1, :].rearrange("p m f -> p (m f)"),
             )
 
         def mx(c):
@@ -130,86 +161,94 @@ def tile_cfkanlayer_kernel(tc, x, cheby_coeffs, bias, out):
             )
 
         def w_perm():
-            for h in range(2):
+            for oh in range(2):
                 nc.vector.tensor_copy(
-                    out=w_p[:, h].rearrange("o k (c a i) -> o k c a i", c=4, a=16, i=4),
-                    in_=w_sb[:, h, :].rearrange("o (a c i k) -> o k c a i", a=16, c=4, i=4, k=KD),
+                    out=w_p[:, oh].rearrange("o m (y b i) -> o m y b i", y=8, b=8, i=4),
+                    in_=w_sb[:, oh, :].bitcast(F32).rearrange("o (b y i m) -> o m y b i", b=8, y=8, i=4, m=4),
                 )
 
         def w_rest():
             for m in range(4):
-                w_t = wt_r[m % 2]
-                for s in range(2):
-                    for h in range(2):
+                w_t = acc_r[m]
+                for h in range(2):
+                    for oh in range(2):
                         nc.tensor.transpose(
-                            w_t[:, s, h * P : (h + 1) * P], w_p[:, h, 2 * m + s, :].bitcast(F32), ident[:]
+                            w_t[:, h, oh * P : (oh + 1) * P], w_p[:, oh, m, h * P : (h + 1) * P], ident[:]
                         )
                 nc.scalar.copy(
-                    out=w_g[:, m, :].rearrange("p (o s) -> p o s", s=2),
-                    in_=w_t[:].rearrange("p s o -> p o s"),
+                    out=w_g[:, m, :].rearrange("p (q h) -> p q h", h=2),
+                    in_=w_t[:].bitcast(BF16).rearrange("p h q -> p q h"),
                 )
             nc.vector.quantize_mx(
                 out=w_c[:].rearrange("p m o -> p (m o)").bitcast(FP8X4),
                 scales=w_s[:].rearrange("p m o -> p (m o)"),
-                in_=w_g[:].rearrange("p m f -> p (m f)").bitcast(BF16),
+                in_=w_g[:].rearrange("p m f -> p (m f)"),
             )
             nc.scalar.copy(out=b_f32[:], in_=b_bf[:])
 
-        xperm(0)
-        xtrans(0)
-        xperm(1)
-        xtrans(1)
-        nc.vector.memset(g0_r[0][:], 1.0)
-        nc.vector.memset(g0_r[1][:], 1.0)
+        tanh(0)
+        ttrans(0)
+        nc.vector.memset(g_r[0][:, 0, :], 1.0)
+        nc.vector.memset(g_r[1][:, 0, :], 1.0)
         w_perm()
 
         for i in range(NCH + 3):
             a, b, c, d = i, i - 1, i - 2, i - 3
-            if ok(a):
-                act(t_r[a % 2][:], xt_r[a % 2][:].bitcast(BF16), ACTF.Tanh)
             if ok(b):
-                act(sq_r[b % 2][:, 2, :], t3_r[b % 2][:], ACTF.Square, scale=2.0)
-            if ok(a):
-                act(sq_r[a % 2][:, 0, :], t_r[a % 2][:], ACTF.Square, scale=2.0)
-            if ok(b):
-                act(pl_r[b % 2][:, :, 0, :], sq_r[b % 2][:], ACTF.Identity, scale=0.5, bias_=-1.0)
-            if ok(a):
-                act(sq_r[a % 2][:, 1, :], sq_r[a % 2][:, 0, :], ACTF.Square, bias_=-2.0)
-            if ok(b):
-                nc.scalar.copy(
-                    out=g0_r[b % 2][:].rearrange("p (n s e) -> p n s e", s=2, e=2)[:, :, 1, :],
-                    in_=t_r[b % 2][:].rearrange("p (n e) -> p n e", e=2),
-                )
-            if ok(a):
-                act(q5_r[a % 2][:], sq_r[a % 2][:, 0, :], ACTF.Square, bias_=-2.5)
-            if ok(a + 1) and a + 1 >= 2:
-                xperm(a + 1)
-                xtrans(a + 1)
+                for g in range(2):
+                    nc.scalar.copy(
+                        out=g_r[b % 2][:, 0, :].rearrange("p (g n s h) -> p g n s h", g=2, s=2, h=2)[:, g, :, 1, :],
+                        in_=nh(t_ps(b))[:, g],
+                    )
             if ok(c):
-                regroup(c, 0, 2)
-                regroup(c, 2, 3)
-            if ok(b):
-                stt(mm_r[0][:], sq_r[b % 2][:, 1, :], 2.0, t3_r[b % 2][:])
-            if ok(c):
-                quant(c, 1, 2)
-            if ok(b):
-                nc.vector.tensor_tensor(
-                    out=pl_r[b % 2][:, 2, 1, :], in0=mm_r[0][:], in1=t_r[b % 2][:], op=ALU.subtract
-                )
-            if ok(c):
-                quant(c, 0, 1)
-                quant(c, 2, 4)
-                mx(c)
-            if ok(b):
-                stt(pl_r[b % 2][:, 1, 1, :], q5_r[b % 2][:], 1.25, t_r[b % 2][:])
+                regroup(c, 1)
             if ok(a):
-                stt(t3_r[a % 2][:], sq_r[a % 2][:, 0, :], 3.0, t_r[a % 2][:])
-                nc.gpsimd.tensor_scalar(
-                    out=pl_r[a % 2][:, 0, 1, :], in0=t3_r[a % 2][:], scalar1=1.0, scalar2=0.0, op0=ALU.mult, op1=ALU.add
-                )
+                for g in range(2):
+                    act(half(z_r[a % 2][:], g), half(t_ps(a), g), ACTF.Square, scale=2.0)
+            if ok(c):
+                regroup(c, 3)
+            if ok(b):
+                act(w6_r[b % 2][:], t3_r[b % 2][:], ACTF.Square, scale=2.0)
+            if ok(a + 1):
+                tanh(a + 1)
+            if ok(a):
+                act(v4_r[a % 2][:], z_r[a % 2][:], ACTF.Square, bias_=-2.0)
+                act(q5_r[a % 2][:], z_r[a % 2][:], ACTF.Square, bias_=-2.5)
             if i == 0:
                 w_rest()
+            if ok(b):
+                stt(mm_r[0][:], v4_r[b % 2][:], 2.0, t3_r[b % 2][:])
+            if ok(c):
+                for m in range(1, 4):
+                    if m not in SRG:
+                        regroup(c, m)
+            if ok(b):
+                for g in range(2):
+                    nc.vector.tensor_tensor(
+                        out=gnh(pl(b, 3, 1))[:, g], in0=nh(mm_r[0][:])[:, g], in1=nh(t_ps(b))[:, g], op=ALU.subtract
+                    )
+                for g in range(2):
+                    stt(
+                        gnh(pl(b, 2, 1))[:, g],
+                        nh(q5_r[b % 2][:])[:, g],
+                        1.25,
+                        nh(t_ps(b))[:, g],
+                    )
+                gaff(pl(b, 2, 0), v4_r[b % 2][:], 0.5, -1.0)
+                gaff(pl(b, 1, 0), z_r[b % 2][:], 0.5, -1.0)
+                gaff(pl(b, 3, 0), w6_r[b % 2][:], 0.5, -1.0)
+                gaff(pl(b, 1, 1), t3_r[b % 2][:], 1.0, 0.0)
+            if ok(a):
+                for g in range(2):
+                    stt(half(t3_r[a % 2][:], g), half(z_r[a % 2][:], g), 3.0, half(t_ps(a), g))
+            if ok(a + 1):
+                ttrans(a + 1)
             if ok(d):
                 outp(d, 0)
                 outp(d, 1)
                 nc.sync.dma_start(out=out_v[:, d * CH : (d + 1) * CH, :], in_=o_r[d % 2][:])
+            if ok(c):
+                quant(c, 0, 1)
+                quant(c, 1, 2)
+                quant(c, 2, 4)
+                mx(c)

@@ -194,6 +194,10 @@ def tile_cfkanlayer_kernel(tc, x, cheby_coeffs, bias, out):
 
         for i in range(NCH + 3):
             a, b, c, d = i, i - 1, i - 2, i - 3
+            if ok(c):
+                nc.vector.tensor_scalar(
+                    out=gnh(pl(c, 3, 0)), in0=nh(w6_r[c % 2][:]), scalar1=0.5, scalar2=-1.0, op0=ALU.mult, op1=ALU.add
+                )
             if ok(b):
                 for g in range(2):
                     nc.scalar.copy(
@@ -236,7 +240,6 @@ def tile_cfkanlayer_kernel(tc, x, cheby_coeffs, bias, out):
                     )
                 gaff(pl(b, 2, 0), v4_r[b % 2][:], 0.5, -1.0)
                 gaff(pl(b, 1, 0), z_r[b % 2][:], 0.5, -1.0)
-                gaff(pl(b, 3, 0), w6_r[b % 2][:], 0.5, -1.0)
                 gaff(pl(b, 1, 1), t3_r[b % 2][:], 1.0, 0.0)
             if ok(a):
                 for g in range(2):

@@ -52,13 +52,13 @@ def tile_cfkanlayer_kernel(tc, x, cheby_coeffs, bias, out):
         make_identity(nc, ident[:])
 
         tn_r = ring(2, [P, CH, D_IN], F32, "tn")
-        z_r = ring(2, [P, FD], F32, "z")
-        v4_r = ring(2, [P, FD], F32, "v4")
+        zv_r = ring(2, [P, 2, FD], F32, "zv")
         w6_r = ring(2, [P, FD], F32, "w6")
         q5_r = ring(2, [P, FD], F32, "q5")
         t3_r = ring(2, [P, FD], F32, "t3")
         mm_r = ring(1, [P, FD], F32, "mm")
-        pl_r = [ring(1 if m == 2 else 2, [P, 2, FD], BF16, "pl%d" % m) for m in range(1, 4)]
+        pa_r = ring(1, [P, 2, 2, FD], BF16, "pa")
+        pb_r = ring(2, [P, 2, FD], BF16, "pb")
         g_r = ring(2, [P, 4, 2 * FD], BF16, "g", align=64)
         cod_r = ring(2, [P, 4, CT], U32, "cod", align=64)
         scl_r = ring(2, [P, 4, CT], U8, "scl", align=64)
@@ -109,14 +109,17 @@ def tile_cfkanlayer_kernel(tc, x, cheby_coeffs, bias, out):
         def stt(o, a, s, b):
             nc.vector.scalar_tensor_tensor(out=o, in0=a, scalar=s, in1=b, op0=ALU.subtract, op1=ALU.mult)
 
-        def gaff(o, i, s, b):
-            nc.gpsimd.tensor_scalar(out=gnh(o), in0=nh(i), scalar1=s, scalar2=b, op0=ALU.mult, op1=ALU.add)
+        def pl(c, m):
+            return pb_r[c % 2][:] if m == 3 else pa_r[0][:, :, m - 1, :]
 
-        def pl(c, m, s):
-            return pl_r[m - 1][c % len(pl_r[m - 1])][:, s, :]
+        def z(c):
+            return zv_r[c % 2][:, 0, :]
+
+        def v4(c):
+            return zv_r[c % 2][:, 1, :]
 
         def regroup(c, m):
-            src = pl_r[m - 1][c % len(pl_r[m - 1])][:]
+            src = pl(c, m)
             dst = g_r[c % 2][:, m, :]
             if m in SRG:
                 nc.scalar.copy(
@@ -167,24 +170,34 @@ def tile_cfkanlayer_kernel(tc, x, cheby_coeffs, bias, out):
                     in_=w_sb[:, oh, :].bitcast(F32).rearrange("o (b y i m) -> o m y b i", b=8, y=8, i=4, m=4),
                 )
 
+        def w_copy(m, s, word, half_):
+            nc.vector.tensor_copy(
+                out=w_g[:, m, :].rearrange("p (o s h) -> p o s h", s=2, h=2)[:, :, s, :],
+                in_=acc_r[word][:].bitcast(BF16).rearrange("p h (o s) -> p o s h", s=2)[:, :, half_, :],
+            )
+
         def w_rest():
             for m in range(4):
-                w_t = acc_r[m]
                 for h in range(2):
                     for oh in range(2):
                         nc.tensor.transpose(
-                            w_t[:, h, oh * P : (oh + 1) * P], w_p[:, oh, m, h * P : (h + 1) * P], ident[:]
+                            acc_r[m][:, h, oh * P : (oh + 1) * P], w_p[:, oh, m, h * P : (h + 1) * P], ident[:]
                         )
-                nc.scalar.copy(
+            w_copy(0, 0, 0, 0)
+            w_copy(1, 1, 0, 1)
+            w_copy(1, 0, 1, 0)
+            w_copy(0, 1, 1, 1)
+            for m in range(2, 4):
+                nc.vector.tensor_copy(
                     out=w_g[:, m, :].rearrange("p (q h) -> p q h", h=2),
-                    in_=w_t[:].bitcast(BF16).rearrange("p h q -> p q h"),
+                    in_=acc_r[m][:].bitcast(BF16).rearrange("p h q -> p q h"),
                 )
             nc.vector.quantize_mx(
                 out=w_c[:].rearrange("p m o -> p (m o)").bitcast(FP8X4),
                 scales=w_s[:].rearrange("p m o -> p (m o)"),
                 in_=w_g[:].rearrange("p m f -> p (m f)"),
             )
-            nc.scalar.copy(out=b_f32[:], in_=b_bf[:])
+            nc.gpsimd.tensor_copy(out=b_f32[:], in_=b_bf[:])
 
         tanh(0)
         ttrans(0)
@@ -196,19 +209,19 @@ def tile_cfkanlayer_kernel(tc, x, cheby_coeffs, bias, out):
             a, b, c, d = i, i - 1, i - 2, i - 3
             if ok(c):
                 nc.vector.tensor_scalar(
-                    out=gnh(pl(c, 3, 0)), in0=nh(w6_r[c % 2][:]), scalar1=0.5, scalar2=-1.0, op0=ALU.mult, op1=ALU.add
+                    out=gnh(pl(c, 3)[:, 0, :]), in0=nh(w6_r[c % 2][:]), scalar1=0.5, scalar2=-1.0, op0=ALU.mult, op1=ALU.add
                 )
+            if ok(c):
+                regroup(c, 1)
             if ok(b):
                 for g in range(2):
                     nc.scalar.copy(
-                        out=g_r[b % 2][:, 0, :].rearrange("p (g n s h) -> p g n s h", g=2, s=2, h=2)[:, g, :, 1, :],
+                        out=gnh(pl(b, 1)[:, 1, :])[:, g],
                         in_=nh(t_ps(b))[:, g],
                     )
-            if ok(c):
-                regroup(c, 1)
             if ok(a):
                 for g in range(2):
-                    act(half(z_r[a % 2][:], g), half(t_ps(a), g), ACTF.Square, scale=2.0)
+                    act(half(z(a), g), half(t_ps(a), g), ACTF.Square, scale=2.0)
             if ok(c):
                 regroup(c, 3)
             if ok(b):
@@ -216,12 +229,10 @@ def tile_cfkanlayer_kernel(tc, x, cheby_coeffs, bias, out):
             if ok(a + 1):
                 tanh(a + 1)
             if ok(a):
-                act(v4_r[a % 2][:], z_r[a % 2][:], ACTF.Square, bias_=-2.0)
-                act(q5_r[a % 2][:], z_r[a % 2][:], ACTF.Square, bias_=-2.5)
-            if i == 0:
-                w_rest()
+                act(v4(a), z(a), ACTF.Square, bias_=-2.0)
+                act(q5_r[a % 2][:], z(a), ACTF.Square, bias_=-2.5)
             if ok(b):
-                stt(mm_r[0][:], v4_r[b % 2][:], 2.0, t3_r[b % 2][:])
+                stt(mm_r[0][:], v4(b), 2.0, t3_r[b % 2][:])
             if ok(c):
                 for m in range(1, 4):
                     if m not in SRG:
@@ -229,21 +240,36 @@ def tile_cfkanlayer_kernel(tc, x, cheby_coeffs, bias, out):
             if ok(b):
                 for g in range(2):
                     nc.vector.tensor_tensor(
-                        out=gnh(pl(b, 3, 1))[:, g], in0=nh(mm_r[0][:])[:, g], in1=nh(t_ps(b))[:, g], op=ALU.subtract
+                        out=gnh(pl(b, 3)[:, 1, :])[:, g], in0=nh(mm_r[0][:])[:, g], in1=nh(t_ps(b))[:, g], op=ALU.subtract
                     )
                 for g in range(2):
                     stt(
-                        gnh(pl(b, 2, 1))[:, g],
+                        gnh(pl(b, 2)[:, 1, :])[:, g],
                         nh(q5_r[b % 2][:])[:, g],
                         1.25,
                         nh(t_ps(b))[:, g],
                     )
-                gaff(pl(b, 2, 0), v4_r[b % 2][:], 0.5, -1.0)
-                gaff(pl(b, 1, 0), z_r[b % 2][:], 0.5, -1.0)
-                gaff(pl(b, 1, 1), t3_r[b % 2][:], 1.0, 0.0)
+                nc.gpsimd.tensor_scalar(
+                    out=pa_r[0][:, 0].rearrange("p m (g n h) -> p (m g) n h", g=2, h=2),
+                    in0=zv_r[b % 2][:].rearrange("p m (g h n) -> p (m g) n h", g=2, h=2),
+                    scalar1=0.5,
+                    scalar2=-1.0,
+                    op0=ALU.mult,
+                    op1=ALU.add,
+                )
+                nc.gpsimd.tensor_scalar(
+                    out=g_r[b % 2][:, 0, :].rearrange("p (g n s h) -> p g n s h", g=2, s=2, h=2)[:, :, :, 1, :],
+                    in0=nh(t3_r[b % 2][:]),
+                    scalar1=1.0,
+                    scalar2=0.0,
+                    op0=ALU.mult,
+                    op1=ALU.add,
+                )
             if ok(a):
                 for g in range(2):
-                    stt(half(t3_r[a % 2][:], g), half(z_r[a % 2][:], g), 3.0, half(t_ps(a), g))
+                    stt(half(t3_r[a % 2][:], g), half(z(a), g), 3.0, half(t_ps(a), g))
+            if i == 0:
+                w_rest()
             if ok(a + 1):
                 ttrans(a + 1)
             if ok(d):

@@ -80,9 +80,6 @@ def tile_cfkanlayer_kernel(tc, x, cheby_coeffs, bias, out):
         def t_ps(c):
             return tp_r[c % 2][:].rearrange("p g h n -> p (g h n)")
 
-        def half(ap, g):
-            return ap[:, g * (FD // 2) : (g + 1) * (FD // 2)]
-
         def nh(ap):
             return ap.rearrange("p (g h n) -> p g n h", g=2, h=2)
 
@@ -188,7 +185,7 @@ def tile_cfkanlayer_kernel(tc, x, cheby_coeffs, bias, out):
             w_copy(1, 0, 1, 0)
             w_copy(0, 1, 1, 1)
             for m in range(2, 4):
-                nc.vector.tensor_copy(
+                nc.scalar.copy(
                     out=w_g[:, m, :].rearrange("p (q h) -> p q h", h=2),
                     in_=acc_r[m][:].bitcast(BF16).rearrange("p h q -> p q h"),
                 )
@@ -209,7 +206,7 @@ def tile_cfkanlayer_kernel(tc, x, cheby_coeffs, bias, out):
             a, b, c, d = i, i - 1, i - 2, i - 3
             if ok(c):
                 nc.vector.tensor_scalar(
-                    out=gnh(pl(c, 3)[:, 0, :]), in0=nh(w6_r[c % 2][:]), scalar1=0.5, scalar2=-1.0, op0=ALU.mult, op1=ALU.add
+                    out=pl(c, 3)[:, 0, :], in0=w6_r[c % 2][:], scalar1=0.5, scalar2=-1.0, op0=ALU.mult, op1=ALU.add
                 )
             if ok(c):
                 regroup(c, 1)
@@ -221,7 +218,7 @@ def tile_cfkanlayer_kernel(tc, x, cheby_coeffs, bias, out):
                     )
             if ok(a):
                 for g in range(2):
-                    act(half(z(a), g), half(t_ps(a), g), ACTF.Square, scale=2.0)
+                    act(gnh(z(a))[:, g], nh(t_ps(a))[:, g], ACTF.Square, scale=2.0)
             if ok(c):
                 regroup(c, 3)
             if ok(b):
@@ -240,18 +237,18 @@ def tile_cfkanlayer_kernel(tc, x, cheby_coeffs, bias, out):
             if ok(b):
                 for g in range(2):
                     nc.vector.tensor_tensor(
-                        out=gnh(pl(b, 3)[:, 1, :])[:, g], in0=nh(mm_r[0][:])[:, g], in1=nh(t_ps(b))[:, g], op=ALU.subtract
+                        out=gnh(pl(b, 3)[:, 1, :])[:, g], in0=gnh(mm_r[0][:])[:, g], in1=nh(t_ps(b))[:, g], op=ALU.subtract
                     )
                 for g in range(2):
                     stt(
                         gnh(pl(b, 2)[:, 1, :])[:, g],
-                        nh(q5_r[b % 2][:])[:, g],
+                        gnh(q5_r[b % 2][:])[:, g],
                         1.25,
                         nh(t_ps(b))[:, g],
                     )
                 nc.gpsimd.tensor_scalar(
-                    out=pa_r[0][:, 0].rearrange("p m (g n h) -> p (m g) n h", g=2, h=2),
-                    in0=zv_r[b % 2][:].rearrange("p m (g h n) -> p (m g) n h", g=2, h=2),
+                    out=pa_r[0][:, 0],
+                    in0=zv_r[b % 2][:],
                     scalar1=0.5,
                     scalar2=-1.0,
                     op0=ALU.mult,
@@ -259,7 +256,7 @@ def tile_cfkanlayer_kernel(tc, x, cheby_coeffs, bias, out):
                 )
                 nc.gpsimd.tensor_scalar(
                     out=g_r[b % 2][:, 0, :].rearrange("p (g n s h) -> p g n s h", g=2, s=2, h=2)[:, :, :, 1, :],
-                    in0=nh(t3_r[b % 2][:]),
+                    in0=gnh(t3_r[b % 2][:]),
                     scalar1=1.0,
                     scalar2=0.0,
                     op0=ALU.mult,
@@ -267,7 +264,7 @@ def tile_cfkanlayer_kernel(tc, x, cheby_coeffs, bias, out):
                 )
             if ok(a):
                 for g in range(2):
-                    stt(half(t3_r[a % 2][:], g), half(z(a), g), 3.0, half(t_ps(a), g))
+                    stt(gnh(t3_r[a % 2][:])[:, g], gnh(z(a))[:, g], 3.0, nh(t_ps(a))[:, g])
             if i == 0:
                 w_rest()
             if ok(a + 1):

@@ -17,11 +17,12 @@ D_IN = 256
 KD = 8
 D_OUT = 256
 NT = N_TOK // P
-CH = 4
-NCH = NT // CH
-CT = CH * P
-FD = CT * 2
-SRG = (1, 3)
+GP = 2
+GE = 2 * GP * P
+NG = (1,) + (2,) * 15 + (1,)
+NCH = len(NG)
+T0 = [GP * sum(NG[:c]) for c in range(NCH)]
+FD = max(NG) * GE
 FLOPS = 2 * N_TOK * D_OUT * D_IN * KD
 
 
@@ -42,29 +43,31 @@ def tile_cfkanlayer_kernel(tc, x, cheby_coeffs, bias, out):
         x_sb = keep.tile([P, NT, D_IN], BF16)
         w_sb = keep.tile([P, 2, D_IN * KD], BF16)
         b_bf = keep.tile([P, D_OUT], BF16)
-        nc.sync.dma_start(out=x_sb[:, 0:8, :], in_=x_v[:, 0:8, :])
+        nc.sync.dma_start(out=x_sb[:, 0:2, :], in_=x_v[:, 0:2, :])
         nc.sync.dma_start(out=w_sb[:], in_=cheby_coeffs.rearrange("(h o) d k -> o h (d k)", h=2))
+        for lo, hi in ((2, 6), (6, 14)):
+            nc.sync.dma_start(out=x_sb[:, lo:hi, :], in_=x_v[:, lo:hi, :])
         nc.sync.dma_start(out=b_bf[:], in_=bias.rearrange("a o -> (a o)").partition_broadcast(P))
-        for lo, hi in ((8, 16), (16, 32), (32, 64)):
+        for lo, hi in ((14, 30), (30, 64)):
             nc.sync.dma_start(out=x_sb[:, lo:hi, :], in_=x_v[:, lo:hi, :])
 
         ident = keep.tile([P, P], F32)
         make_identity(nc, ident[:])
 
-        tn_r = ring(2, [P, CH, D_IN], F32, "tn")
-        zv_r = ring(2, [P, 2, FD], F32, "zv")
-        w6_r = ring(2, [P, FD], F32, "w6")
+        tn_r = ring(2, [P, 2 * GP, D_IN], F32, "tn")
+        z_r = ring(2, [P, FD], F32, "z")
+        vw_r = ring(2, [P, 2, FD], F32, "vw")
         q5_r = ring(2, [P, FD], F32, "q5")
         t3_r = ring(2, [P, FD], F32, "t3")
         mm_r = ring(1, [P, FD], F32, "mm")
-        pa_r = ring(1, [P, 2, 2, FD], BF16, "pa")
-        pb_r = ring(2, [P, 2, FD], BF16, "pb")
-        g_r = ring(2, [P, 4, 2 * FD], BF16, "g", align=64)
-        cod_r = ring(2, [P, 4, CT], U32, "cod", align=64)
-        scl_r = ring(2, [P, 4, CT], U8, "scl", align=64)
-        o_r = ring(2, [P, CH, D_OUT], F32, "o")
-        tp_r = ring(2, [P, 2, 2, 2 * P], F32, "tp", pool=ps)
-        acc_r = ring(4, [P, 2, D_OUT], F32, "acc", pool=ps)
+        pl_r = ring(2, [P, 2, 2, FD], BF16, "pl")
+        g0_r = ring(1, [P, 2 * FD], BF16, "g0", align=64)
+        g_r = ring(2, [P, 3, 2 * FD], BF16, "g", align=64)
+        cod_r = ring(2, [P, 4, FD // 2], U32, "cod", align=64)
+        scl_r = ring(2, [P, 4, FD // 2], U8, "scl", align=64)
+        o_r = ring(2, [P, 2 * GP, D_OUT], F32, "o")
+        tp_r = ring(4, [P, 2, GP * P], F32, "tp", pool=ps)
+        acc_r = ring(4, [P, GP, D_OUT], F32, "acc", pool=ps)
         b_f32 = keep.tile([P, D_OUT], F32)
         w_p = keep.tile([P, 2, KD // 2, D_IN], F32)
         w_g = keep.tile([P, 4, 4 * D_OUT], BF16, align_bytes=64)
@@ -74,31 +77,64 @@ def tile_cfkanlayer_kernel(tc, x, cheby_coeffs, bias, out):
         def ok(c):
             return 0 <= c < NCH
 
+        def groups(c):
+            return range(NG[c])
+
+        def fd(c):
+            return NG[c] * GE
+
+        def nh(ap, g):
+            return ap[:, g * GE : (g + 1) * GE].rearrange("p (n h) -> p n h", h=2)
+
+        def t_ps(c, g):
+            return tp_r[2 * (c % 2) + g][:].rearrange("p h n -> p n h")
+
+        def z(c):
+            return z_r[c % 2][:, 0 : fd(c)]
+
+        def v4(c):
+            return vw_r[c % 2][:, 0, 0 : fd(c)]
+
+        def q5(c):
+            return q5_r[c % 2][:, 0 : fd(c)]
+
+        def t3(c):
+            return t3_r[c % 2][:, 0 : fd(c)]
+
+        def w6(c):
+            return vw_r[c % 2][:, 1, 0 : fd(c)]
+
+        def mm(c):
+            return mm_r[0][:, 0 : fd(c)]
+
+        def odd(c, m):
+            return pl_r[c % 2][:, 1, m - 2, 0 : fd(c)]
+
+        def grouped(c, m):
+            return g0_r[0][:, 0 : 2 * fd(c)] if m == 0 else g_r[c % 2][:, m - 1, 0 : 2 * fd(c)]
+
+        def slot(c, m, s):
+            return grouped(c, m).rearrange("p (n s h) -> p n s h", s=2, h=2)[:, :, s, :]
+
+        def slot_g(c, m, s, g):
+            return slot(c, m, s)[:, g * GP * P : (g + 1) * GP * P]
+
         def act(o, i, f, scale=1.0, bias_=0.0):
             nc.scalar.activation(out=o, in_=i, func=f, scale=scale, bias=bias_)
 
-        def t_ps(c):
-            return tp_r[c % 2][:].rearrange("p g h n -> p (g h n)")
-
-        def nh(ap):
-            return ap.rearrange("p (g h n) -> p g n h", g=2, h=2)
-
-        def gnh(ap):
-            return ap.rearrange("p (g n h) -> p g n h", g=2, h=2)
-
         def tanh(c):
-            for tl in range(CH):
+            for tl in range(GP * NG[c]):
                 act(
                     tn_r[c % 2][:, tl, :].rearrange("p (y b i) -> p y b i", y=8, b=8, i=4),
-                    x_sb[:, c * CH + tl, :].rearrange("p (b y i) -> p y b i", y=8, b=8, i=4),
+                    x_sb[:, T0[c] + tl, :].rearrange("p (b y i) -> p y b i", y=8, b=8, i=4),
                     ACTF.Tanh,
                 )
 
         def ttrans(c):
-            for tl in range(CH):
+            for tl in range(GP * NG[c]):
                 for h in range(2):
                     nc.tensor.transpose(
-                        tp_r[c % 2][:, tl // 2, h, (tl % 2) * P : (tl % 2 + 1) * P],
+                        tp_r[2 * (c % 2) + tl // GP][:, h, (tl % GP) * P : (tl % GP + 1) * P],
                         tn_r[c % 2][:, tl, h * P : (h + 1) * P],
                         ident[:],
                     )
@@ -106,44 +142,34 @@ def tile_cfkanlayer_kernel(tc, x, cheby_coeffs, bias, out):
         def stt(o, a, s, b):
             nc.vector.scalar_tensor_tensor(out=o, in0=a, scalar=s, in1=b, op0=ALU.subtract, op1=ALU.mult)
 
-        def pl(c, m):
-            return pb_r[c % 2][:] if m == 3 else pa_r[0][:, :, m - 1, :]
+        def affine(eng, o, i, s, b):
+            eng.tensor_scalar(out=o, in0=i, scalar1=s, scalar2=b, op0=ALU.mult, op1=ALU.add)
 
-        def z(c):
-            return zv_r[c % 2][:, 0, :]
-
-        def v4(c):
-            return zv_r[c % 2][:, 1, :]
-
-        def regroup(c, m):
-            src = pl(c, m)
-            dst = g_r[c % 2][:, m, :]
-            if m in SRG:
-                nc.scalar.copy(
-                    out=dst.bitcast(F32).rearrange("p (n s) -> p n s", s=2),
-                    in_=src.bitcast(F32).rearrange("p s n -> p n s"),
-                )
-            else:
-                nc.vector.tensor_copy(
-                    out=dst.rearrange("p (n s e) -> p n s e", s=2, e=2),
-                    in_=src.rearrange("p s (n e) -> p n s e", e=2),
-                )
+        def regroup_s(c):
+            nc.scalar.copy(
+                out=g_r[c % 2][:, 1:3, 0 : 2 * fd(c)].bitcast(F32).rearrange("p m (n s) -> p m n s", s=2),
+                in_=pl_r[c % 2][:, :, :, 0 : fd(c)].bitcast(F32).rearrange("p s m n -> p m n s"),
+            )
 
         def quant(c, m0, m1):
+            if NG[c] < max(NG) and m1 - m0 > 1:
+                for m in range(m0, m1):
+                    quant(c, m, m + 1)
+                return
+            n = fd(c) // 2
             nc.vector.quantize_mx(
-                out=cod_r[c % 2][:, m0:m1, :].rearrange("p m n -> p (m n)").bitcast(FP8X4),
-                scales=scl_r[c % 2][:, m0:m1, :].rearrange("p m n -> p (m n)"),
-                in_=g_r[c % 2][:, m0:m1, :].rearrange("p m f -> p (m f)"),
+                out=cod_r[c % 2][:, m0:m1, 0:n].rearrange("p m n -> p (m n)").bitcast(FP8X4),
+                scales=scl_r[c % 2][:, m0:m1, 0:n].rearrange("p m n -> p (m n)"),
+                in_=grouped(c, m0) if m1 - m0 == 1 else g_r[c % 2][:, m0 - 1 : m1 - 1, :].rearrange("p m f -> p (m f)"),
             )
 
         def mx(c):
-            for hp in range(CH // 2):
-                acc = acc_r[2 * (c % 2) + hp]
-                for j in range(2):
-                    cols = slice((2 * hp + j) * P, (2 * hp + j + 1) * P)
+            for g in groups(c):
+                for j in range(GP):
+                    cols = slice((GP * g + j) * P, (GP * g + j + 1) * P)
                     for m in range(4):
                         nc.tensor.matmul_mx(
-                            out=acc[:, j, :],
+                            out=acc_r[2 * (c % 2) + g][:, j, :],
                             lhsT=cod_r[c % 2][:, m, cols].bitcast(FP8X4),
                             lhsT_scale=scl_r[c % 2][:, m, cols],
                             rhs=w_c[:, m, :].bitcast(FP8X4),
@@ -152,13 +178,16 @@ def tile_cfkanlayer_kernel(tc, x, cheby_coeffs, bias, out):
                             stop=(m == 3),
                         )
 
-        def outp(c, hp):
-            nc.vector.tensor_tensor(
-                out=o_r[c % 2][:, 2 * hp : 2 * hp + 2, :],
-                in0=acc_r[2 * (c % 2) + hp][:],
-                in1=b_f32[:].unsqueeze(1).to_broadcast([P, 2, D_OUT]),
-                op=ALU.add,
-            )
+        def outp(c):
+            for g in groups(c):
+                nc.vector.tensor_tensor(
+                    out=o_r[c % 2][:, GP * g : GP * (g + 1), :],
+                    in0=acc_r[2 * (c % 2) + g][:],
+                    in1=b_f32[:].unsqueeze(1).to_broadcast([P, GP, D_OUT]),
+                    op=ALU.add,
+                )
+            nt = GP * NG[c]
+            nc.sync.dma_start(out=out_v[:, T0[c] : T0[c] + nt, :], in_=o_r[c % 2][:, 0:nt, :])
 
         def w_perm():
             for oh in range(2):
@@ -198,83 +227,49 @@ def tile_cfkanlayer_kernel(tc, x, cheby_coeffs, bias, out):
 
         tanh(0)
         ttrans(0)
-        nc.vector.memset(g_r[0][:, 0, :], 1.0)
-        nc.vector.memset(g_r[1][:, 0, :], 1.0)
+        nc.vector.memset(g0_r[0][:], 1.0)
         w_perm()
 
         for i in range(NCH + 3):
             a, b, c, d = i, i - 1, i - 2, i - 3
             if ok(c):
-                nc.vector.tensor_scalar(
-                    out=pl(c, 3)[:, 0, :], in0=w6_r[c % 2][:], scalar1=0.5, scalar2=-1.0, op0=ALU.mult, op1=ALU.add
-                )
-            if ok(c):
-                regroup(c, 1)
+                affine(nc.vector, pl_r[c % 2][:, 0, :, 0 : fd(c)], vw_r[c % 2][:, :, 0 : fd(c)], 0.5, -1.0)
             if ok(b):
-                for g in range(2):
-                    nc.scalar.copy(
-                        out=gnh(pl(b, 1)[:, 1, :])[:, g],
-                        in_=nh(t_ps(b))[:, g],
-                    )
+                for g in groups(b):
+                    nc.scalar.copy(out=slot_g(b, 1, 1, g), in_=t_ps(b, g))
             if ok(a):
-                for g in range(2):
-                    act(gnh(z(a))[:, g], nh(t_ps(a))[:, g], ACTF.Square, scale=2.0)
-            if ok(c):
-                regroup(c, 3)
+                for g in groups(a):
+                    act(nh(z(a), g), t_ps(a, g), ACTF.Square, scale=2.0)
             if ok(b):
-                act(w6_r[b % 2][:], t3_r[b % 2][:], ACTF.Square, scale=2.0)
+                act(w6(b), t3(b), ACTF.Square, scale=2.0)
+            if ok(c):
+                regroup_s(c)
             if ok(a + 1):
                 tanh(a + 1)
             if ok(a):
                 act(v4(a), z(a), ACTF.Square, bias_=-2.0)
-                act(q5_r[a % 2][:], z(a), ACTF.Square, bias_=-2.5)
+                act(q5(a), z(a), ACTF.Square, bias_=-2.5)
             if ok(b):
-                stt(mm_r[0][:], v4(b), 2.0, t3_r[b % 2][:])
+                stt(mm(b), v4(b), 2.0, t3(b))
             if ok(c):
-                for m in range(1, 4):
-                    if m not in SRG:
-                        regroup(c, m)
+                quant(c, 0, 1)
             if ok(b):
-                for g in range(2):
-                    nc.vector.tensor_tensor(
-                        out=gnh(pl(b, 3)[:, 1, :])[:, g], in0=gnh(mm_r[0][:])[:, g], in1=nh(t_ps(b))[:, g], op=ALU.subtract
-                    )
-                for g in range(2):
-                    stt(
-                        gnh(pl(b, 2)[:, 1, :])[:, g],
-                        gnh(q5_r[b % 2][:])[:, g],
-                        1.25,
-                        nh(t_ps(b))[:, g],
-                    )
-                nc.gpsimd.tensor_scalar(
-                    out=pa_r[0][:, 0],
-                    in0=zv_r[b % 2][:],
-                    scalar1=0.5,
-                    scalar2=-1.0,
-                    op0=ALU.mult,
-                    op1=ALU.add,
-                )
-                nc.gpsimd.tensor_scalar(
-                    out=g_r[b % 2][:, 0, :].rearrange("p (g n s h) -> p g n s h", g=2, s=2, h=2)[:, :, :, 1, :],
-                    in0=gnh(t3_r[b % 2][:]),
-                    scalar1=1.0,
-                    scalar2=0.0,
-                    op0=ALU.mult,
-                    op1=ALU.add,
-                )
+                for g in groups(b):
+                    nc.vector.tensor_tensor(out=nh(odd(b, 3), g), in0=nh(mm(b), g), in1=t_ps(b, g), op=ALU.subtract)
+                for g in groups(b):
+                    stt(nh(odd(b, 2), g), nh(q5(b), g), 1.25, t_ps(b, g))
+                affine(nc.gpsimd, slot(b, 0, 1), t3(b).rearrange("p (n h) -> p n h", h=2), 1.0, 0.0)
+                affine(nc.gpsimd, slot(b, 1, 0), z(b).rearrange("p (n h) -> p n h", h=2), 0.5, -1.0)
             if ok(a):
-                for g in range(2):
-                    stt(gnh(t3_r[a % 2][:])[:, g], gnh(z(a))[:, g], 3.0, nh(t_ps(a))[:, g])
+                for g in groups(a):
+                    stt(nh(t3(a), g), nh(z(a), g), 3.0, t_ps(a, g))
             if i == 0:
                 w_rest()
             if ok(a + 1):
                 ttrans(a + 1)
             if ok(d):
-                outp(d, 0)
-                outp(d, 1)
-                nc.sync.dma_start(out=out_v[:, d * CH : (d + 1) * CH, :], in_=o_r[d % 2][:])
+                outp(d)
             if ok(c):
-                quant(c, 0, 1)
                 quant(c, 1, 2)
                 quant(c, 2, 4)
                 mx(c)

@@ -67,7 +67,8 @@ def tile_cfkanlayer_kernel(tc, x, cheby_coeffs, bias, out):
         scl_r = ring(2, [P, 4, FD // 2], U8, "scl", align=64)
         o_r = ring(2, [P, 2 * GP, D_OUT], F32, "o")
         tp_r = ring(4, [P, 2, GP * P], F32, "tp", pool=ps)
-        acc_r = ring(4, [P, GP, D_OUT], F32, "acc", pool=ps)
+        acc_r = ring(2, [P, GP, D_OUT], F32, "acc", pool=ps)
+        t3p_r = ring(2, [P, GE], F32, "t3p", pool=ps)
         b_f32 = keep.tile([P, D_OUT], F32)
         w_p = keep.tile([P, 2, KD // 2, D_IN], F32)
         w_g = keep.tile([P, 4, 4 * D_OUT], BF16, align_bytes=64)
@@ -139,16 +140,32 @@ def tile_cfkanlayer_kernel(tc, x, cheby_coeffs, bias, out):
                         ident[:],
                     )
 
+        def t3_to_psum(c):
+            for g in groups(c):
+                nc.tensor.matmul(
+                    t3p_r[g][:], lhsT=ident[:], rhs=t3(c)[:, g * GE : (g + 1) * GE], start=True, stop=True
+                )
+
         def stt(o, a, s, b):
             nc.vector.scalar_tensor_tensor(out=o, in0=a, scalar=s, in1=b, op0=ALU.subtract, op1=ALU.mult)
 
         def affine(eng, o, i, s, b):
             eng.tensor_scalar(out=o, in0=i, scalar1=s, scalar2=b, op0=ALU.mult, op1=ALU.add)
 
+        def vector_regroups(c):
+            return c % 2 == 1
+
         def regroup_s(c):
+            m0 = 1 if vector_regroups(c) else 0
             nc.scalar.copy(
-                out=g_r[c % 2][:, 1:3, 0 : 2 * fd(c)].bitcast(F32).rearrange("p m (n s) -> p m n s", s=2),
-                in_=pl_r[c % 2][:, :, :, 0 : fd(c)].bitcast(F32).rearrange("p s m n -> p m n s"),
+                out=g_r[c % 2][:, 1 + m0 : 3, 0 : 2 * fd(c)].bitcast(F32).rearrange("p m (n s) -> p m n s", s=2),
+                in_=pl_r[c % 2][:, :, m0:2, 0 : fd(c)].bitcast(F32).rearrange("p s m n -> p m n s"),
+            )
+
+        def regroup_v(c):
+            nc.vector.tensor_copy(
+                out=grouped(c, 2).rearrange("p (n s e) -> p n s e", s=2, e=2),
+                in_=pl_r[c % 2][:, :, 0, 0 : fd(c)].rearrange("p s (n e) -> p n s e", e=2),
             )
 
         def quant(c, m0, m1):
@@ -169,7 +186,7 @@ def tile_cfkanlayer_kernel(tc, x, cheby_coeffs, bias, out):
                     cols = slice((GP * g + j) * P, (GP * g + j + 1) * P)
                     for m in range(4):
                         nc.tensor.matmul_mx(
-                            out=acc_r[2 * (c % 2) + g][:, j, :],
+                            out=acc_r[g][:, j, :],
                             lhsT=cod_r[c % 2][:, m, cols].bitcast(FP8X4),
                             lhsT_scale=scl_r[c % 2][:, m, cols],
                             rhs=w_c[:, m, :].bitcast(FP8X4),
@@ -182,7 +199,7 @@ def tile_cfkanlayer_kernel(tc, x, cheby_coeffs, bias, out):
             for g in groups(c):
                 nc.vector.tensor_tensor(
                     out=o_r[c % 2][:, GP * g : GP * (g + 1), :],
-                    in0=acc_r[2 * (c % 2) + g][:],
+                    in0=acc_r[g][:],
                     in1=b_f32[:].unsqueeze(1).to_broadcast([P, GP, D_OUT]),
                     op=ALU.add,
                 )
@@ -196,10 +213,13 @@ def tile_cfkanlayer_kernel(tc, x, cheby_coeffs, bias, out):
                     in_=w_sb[:, oh, :].bitcast(F32).rearrange("o (b y i m) -> o m y b i", b=8, y=8, i=4, m=4),
                 )
 
+        def w_t(word):
+            return t3p_r[word][:].rearrange("p (h o) -> p h o", h=2) if word < 2 else acc_r[word - 2][:]
+
         def w_copy(m, s, word, half_):
             nc.vector.tensor_copy(
                 out=w_g[:, m, :].rearrange("p (o s h) -> p o s h", s=2, h=2)[:, :, s, :],
-                in_=acc_r[word][:].bitcast(BF16).rearrange("p h (o s) -> p o s h", s=2)[:, :, half_, :],
+                in_=w_t(word).bitcast(BF16).rearrange("p h (o s) -> p o s h", s=2)[:, :, half_, :],
             )
 
         def w_rest():
@@ -207,7 +227,7 @@ def tile_cfkanlayer_kernel(tc, x, cheby_coeffs, bias, out):
                 for h in range(2):
                     for oh in range(2):
                         nc.tensor.transpose(
-                            acc_r[m][:, h, oh * P : (oh + 1) * P], w_p[:, oh, m, h * P : (h + 1) * P], ident[:]
+                            w_t(m)[:, h, oh * P : (oh + 1) * P], w_p[:, oh, m, h * P : (h + 1) * P], ident[:]
                         )
             w_copy(0, 0, 0, 0)
             w_copy(1, 1, 0, 1)
@@ -216,7 +236,7 @@ def tile_cfkanlayer_kernel(tc, x, cheby_coeffs, bias, out):
             for m in range(2, 4):
                 nc.scalar.copy(
                     out=w_g[:, m, :].rearrange("p (q h) -> p q h", h=2),
-                    in_=acc_r[m][:].bitcast(BF16).rearrange("p h q -> p q h"),
+                    in_=w_t(m).bitcast(BF16).rearrange("p h q -> p q h"),
                 )
             nc.vector.quantize_mx(
                 out=w_c[:].rearrange("p m o -> p (m o)").bitcast(FP8X4),
@@ -233,7 +253,7 @@ def tile_cfkanlayer_kernel(tc, x, cheby_coeffs, bias, out):
         for i in range(NCH + 3):
             a, b, c, d = i, i - 1, i - 2, i - 3
             if ok(c):
-                affine(nc.vector, pl_r[c % 2][:, 0, :, 0 : fd(c)], vw_r[c % 2][:, :, 0 : fd(c)], 0.5, -1.0)
+                affine(nc.vector, pl_r[c % 2][:, 0, 1, 0 : fd(c)], w6(c), 0.5, -1.0)
             if ok(b):
                 for g in groups(b):
                     nc.scalar.copy(out=slot_g(b, 1, 1, g), in_=t_ps(b, g))
@@ -249,22 +269,27 @@ def tile_cfkanlayer_kernel(tc, x, cheby_coeffs, bias, out):
             if ok(a):
                 act(v4(a), z(a), ACTF.Square, bias_=-2.0)
                 act(q5(a), z(a), ACTF.Square, bias_=-2.5)
-            if ok(b):
-                stt(mm(b), v4(b), 2.0, t3(b))
             if ok(c):
+                if vector_regroups(c):
+                    regroup_v(c)
                 quant(c, 0, 1)
             if ok(b):
                 for g in groups(b):
-                    nc.vector.tensor_tensor(out=nh(odd(b, 3), g), in0=nh(mm(b), g), in1=t_ps(b, g), op=ALU.subtract)
+                    stt(mm(b)[:, g * GE : (g + 1) * GE], v4(b)[:, g * GE : (g + 1) * GE], 2.0, t3p_r[g][:])
                 for g in groups(b):
                     stt(nh(odd(b, 2), g), nh(q5(b), g), 1.25, t_ps(b, g))
+                for g in groups(b):
+                    nc.vector.tensor_tensor(out=nh(odd(b, 3), g), in0=nh(mm(b), g), in1=t_ps(b, g), op=ALU.subtract)
                 affine(nc.gpsimd, slot(b, 0, 1), t3(b).rearrange("p (n h) -> p n h", h=2), 1.0, 0.0)
                 affine(nc.gpsimd, slot(b, 1, 0), z(b).rearrange("p (n h) -> p n h", h=2), 0.5, -1.0)
+                affine(nc.gpsimd, pl_r[b % 2][:, 0, 0, 0 : fd(b)], v4(b), 0.5, -1.0)
             if ok(a):
                 for g in groups(a):
                     stt(nh(t3(a), g), nh(z(a), g), 3.0, t_ps(a, g))
             if i == 0:
                 w_rest()
+            if ok(a):
+                t3_to_psum(a)
             if ok(a + 1):
                 ttrans(a + 1)
             if ok(d):

@@ -23,6 +23,7 @@ NG = (1,) + (2,) * 15 + (1,)
 NCH = len(NG)
 T0 = [GP * sum(NG[:c]) for c in range(NCH)]
 FD = max(NG) * GE
+PAIRS = ((0, 3), (2, 1), (4, 5), (6, 7))
 FLOPS = 2 * N_TOK * D_OUT * D_IN * KD
 
 
@@ -44,9 +45,9 @@ def tile_cfkanlayer_kernel(tc, x, cheby_coeffs, bias, out):
         w_sb = keep.tile([P, 2, D_IN * KD], BF16)
         b_bf = keep.tile([P, D_OUT], BF16)
         nc.sync.dma_start(out=x_sb[:, 0:2, :], in_=x_v[:, 0:2, :])
+        nc.sync.dma_start(out=x_sb[:, 2:6, :], in_=x_v[:, 2:6, :])
         nc.sync.dma_start(out=w_sb[:], in_=cheby_coeffs.rearrange("(h o) d k -> o h (d k)", h=2))
-        for lo, hi in ((2, 6), (6, 14)):
-            nc.sync.dma_start(out=x_sb[:, lo:hi, :], in_=x_v[:, lo:hi, :])
+        nc.sync.dma_start(out=x_sb[:, 6:14, :], in_=x_v[:, 6:14, :])
         nc.sync.dma_start(out=b_bf[:], in_=bias.rearrange("a o -> (a o)").partition_broadcast(P))
         for lo, hi in ((14, 30), (30, 64)):
             nc.sync.dma_start(out=x_sb[:, lo:hi, :], in_=x_v[:, lo:hi, :])
@@ -61,8 +62,8 @@ def tile_cfkanlayer_kernel(tc, x, cheby_coeffs, bias, out):
         t3_r = ring(2, [P, FD], F32, "t3")
         mm_r = ring(1, [P, FD], F32, "mm")
         pl_r = ring(2, [P, 2, 2, FD], BF16, "pl")
-        g0_r = ring(1, [P, 2 * FD], BF16, "g0", align=64)
-        g_r = ring(2, [P, 3, 2 * FD], BF16, "g", align=64)
+        g01_r = ring(1, [P, 2, 2 * FD], BF16, "g01", align=64)
+        g_r = ring(2, [P, 2, 2 * FD], BF16, "g", align=64)
         cod_r = ring(2, [P, 4, FD // 2], U32, "cod", align=64)
         scl_r = ring(2, [P, 4, FD // 2], U8, "scl", align=64)
         o_r = ring(2, [P, 2 * GP, D_OUT], F32, "o")
@@ -70,8 +71,8 @@ def tile_cfkanlayer_kernel(tc, x, cheby_coeffs, bias, out):
         acc_r = ring(2, [P, GP, D_OUT], F32, "acc", pool=ps)
         t3p_r = ring(2, [P, GE], F32, "t3p", pool=ps)
         b_f32 = keep.tile([P, D_OUT], F32)
-        w_p = keep.tile([P, 2, KD // 2, D_IN], F32)
-        w_g = keep.tile([P, 4, 4 * D_OUT], BF16, align_bytes=64)
+        w_p = keep.tile([P, 2, KD, D_IN], BF16)
+        w_g = keep.tile([P, 4, 2 * D_OUT], F32, align_bytes=64)
         w_c = keep.tile([P, 4, D_OUT], U32, align_bytes=64)
         w_s = keep.tile([P, 4, D_OUT], U8, align_bytes=64)
 
@@ -111,8 +112,11 @@ def tile_cfkanlayer_kernel(tc, x, cheby_coeffs, bias, out):
         def odd(c, m):
             return pl_r[c % 2][:, 1, m - 2, 0 : fd(c)]
 
+        def pair_tile(c, m):
+            return g01_r[0] if m < 2 else g_r[c % 2]
+
         def grouped(c, m):
-            return g0_r[0][:, 0 : 2 * fd(c)] if m == 0 else g_r[c % 2][:, m - 1, 0 : 2 * fd(c)]
+            return pair_tile(c, m)[:, m % 2, 0 : 2 * fd(c)]
 
         def slot(c, m, s):
             return grouped(c, m).rearrange("p (n s h) -> p n s h", s=2, h=2)[:, :, s, :]
@@ -126,8 +130,8 @@ def tile_cfkanlayer_kernel(tc, x, cheby_coeffs, bias, out):
         def tanh(c):
             for tl in range(GP * NG[c]):
                 act(
-                    tn_r[c % 2][:, tl, :].rearrange("p (y b i) -> p y b i", y=8, b=8, i=4),
-                    x_sb[:, T0[c] + tl, :].rearrange("p (b y i) -> p y b i", y=8, b=8, i=4),
+                    tn_r[c % 2][:, tl, :].rearrange("p (c a i) -> p c a i", c=4, a=16, i=4),
+                    x_sb[:, T0[c] + tl, :].rearrange("p (a c i) -> p c a i", c=4, a=16, i=4),
                     ACTF.Tanh,
                 )
 
@@ -136,7 +140,7 @@ def tile_cfkanlayer_kernel(tc, x, cheby_coeffs, bias, out):
                 for h in range(2):
                     nc.tensor.transpose(
                         tp_r[2 * (c % 2) + tl // GP][:, h, (tl % GP) * P : (tl % GP + 1) * P],
-                        tn_r[c % 2][:, tl, h * P : (h + 1) * P],
+                        tn_r[c % 2][:, tl, h : D_IN : 2],
                         ident[:],
                     )
 
@@ -153,12 +157,12 @@ def tile_cfkanlayer_kernel(tc, x, cheby_coeffs, bias, out):
             eng.tensor_scalar(out=o, in0=i, scalar1=s, scalar2=b, op0=ALU.mult, op1=ALU.add)
 
         def vector_regroups(c):
-            return c % 2 == 1
+            return c % 2 == 1 and c < NCH - 3
 
         def regroup_s(c):
             m0 = 1 if vector_regroups(c) else 0
             nc.scalar.copy(
-                out=g_r[c % 2][:, 1 + m0 : 3, 0 : 2 * fd(c)].bitcast(F32).rearrange("p m (n s) -> p m n s", s=2),
+                out=g_r[c % 2][:, m0:2, 0 : 2 * fd(c)].bitcast(F32).rearrange("p m (n s) -> p m n s", s=2),
                 in_=pl_r[c % 2][:, :, m0:2, 0 : fd(c)].bitcast(F32).rearrange("p s m n -> p m n s"),
             )
 
@@ -177,7 +181,7 @@ def tile_cfkanlayer_kernel(tc, x, cheby_coeffs, bias, out):
             nc.vector.quantize_mx(
                 out=cod_r[c % 2][:, m0:m1, 0:n].rearrange("p m n -> p (m n)").bitcast(FP8X4),
                 scales=scl_r[c % 2][:, m0:m1, 0:n].rearrange("p m n -> p (m n)"),
-                in_=grouped(c, m0) if m1 - m0 == 1 else g_r[c % 2][:, m0 - 1 : m1 - 1, :].rearrange("p m f -> p (m f)"),
+                in_=grouped(c, m0) if m1 - m0 == 1 else pair_tile(c, m0)[:].rearrange("p m f -> p (m f)"),
             )
 
         def mx(c):
@@ -206,57 +210,44 @@ def tile_cfkanlayer_kernel(tc, x, cheby_coeffs, bias, out):
             nt = GP * NG[c]
             nc.sync.dma_start(out=out_v[:, T0[c] : T0[c] + nt, :], in_=o_r[c % 2][:, 0:nt, :])
 
-        def w_perm():
-            for oh in range(2):
-                nc.vector.tensor_copy(
-                    out=w_p[:, oh].rearrange("o m (y b i) -> o m y b i", y=8, b=8, i=4),
-                    in_=w_sb[:, oh, :].bitcast(F32).rearrange("o (b y i m) -> o m y b i", b=8, y=8, i=4, m=4),
-                )
-
-        def w_t(word):
-            return t3p_r[word][:].rearrange("p (h o) -> p h o", h=2) if word < 2 else acc_r[word - 2][:]
-
-        def w_copy(m, s, word, half_):
+        def w_perm(oh):
             nc.vector.tensor_copy(
-                out=w_g[:, m, :].rearrange("p (o s h) -> p o s h", s=2, h=2)[:, :, s, :],
-                in_=w_t(word).bitcast(BF16).rearrange("p h (o s) -> p o s h", s=2)[:, :, half_, :],
+                out=w_p[:, oh].rearrange("o k (c a i) -> o k c a i", c=4, a=16, i=4),
+                in_=w_sb[:, oh, :].rearrange("o (a c i k) -> o k c a i", a=16, c=4, i=4, k=KD),
             )
 
-        def w_rest():
+        w_t = (acc_r[0], acc_r[1], t3p_r[1], tp_r[1])
+
+        def w_words(m):
+            return t3p_r[1][:].rearrange("p (s o) -> p s o", s=2) if m == 2 else w_t[m][:]
+
+        def w_trans():
             for m in range(4):
-                for h in range(2):
+                for s in range(2):
                     for oh in range(2):
                         nc.tensor.transpose(
-                            w_t(m)[:, h, oh * P : (oh + 1) * P], w_p[:, oh, m, h * P : (h + 1) * P], ident[:]
+                            w_words(m)[:, s, oh * P : (oh + 1) * P], w_p[:, oh, PAIRS[m][s], :].bitcast(F32), ident[:]
                         )
-            w_copy(0, 0, 0, 0)
-            w_copy(1, 1, 0, 1)
-            w_copy(1, 0, 1, 0)
-            w_copy(0, 1, 1, 1)
-            for m in range(2, 4):
-                nc.scalar.copy(
-                    out=w_g[:, m, :].rearrange("p (q h) -> p q h", h=2),
-                    in_=w_t(m).bitcast(BF16).rearrange("p h q -> p q h"),
-                )
+
+        def w_copy(copy, m):
+            copy(out=w_g[:, m, :].rearrange("p (o s) -> p o s", s=2), in_=w_words(m).rearrange("p s o -> p o s"))
+
+        def w_quant():
             nc.vector.quantize_mx(
                 out=w_c[:].rearrange("p m o -> p (m o)").bitcast(FP8X4),
                 scales=w_s[:].rearrange("p m o -> p (m o)"),
-                in_=w_g[:].rearrange("p m f -> p (m f)"),
+                in_=w_g[:].rearrange("p m f -> p (m f)").bitcast(BF16),
             )
-            nc.gpsimd.tensor_copy(out=b_f32[:], in_=b_bf[:])
 
         tanh(0)
         ttrans(0)
-        nc.vector.memset(g0_r[0][:], 1.0)
-        w_perm()
+        nc.vector.memset(g01_r[0][:, 0, :], 1.0)
+        nc.gpsimd.tensor_copy(out=b_f32[:], in_=b_bf[:])
 
         for i in range(NCH + 3):
             a, b, c, d = i, i - 1, i - 2, i - 3
             if ok(c):
                 affine(nc.vector, pl_r[c % 2][:, 0, 1, 0 : fd(c)], w6(c), 0.5, -1.0)
-            if ok(b):
-                for g in groups(b):
-                    nc.scalar.copy(out=slot_g(b, 1, 1, g), in_=t_ps(b, g))
             if ok(a):
                 for g in groups(a):
                     act(nh(z(a), g), t_ps(a, g), ACTF.Square, scale=2.0)
@@ -266,13 +257,10 @@ def tile_cfkanlayer_kernel(tc, x, cheby_coeffs, bias, out):
                 regroup_s(c)
             if ok(a + 1):
                 tanh(a + 1)
-            if ok(a):
-                act(v4(a), z(a), ACTF.Square, bias_=-2.0)
-                act(q5(a), z(a), ACTF.Square, bias_=-2.5)
             if ok(c):
                 if vector_regroups(c):
                     regroup_v(c)
-                quant(c, 0, 1)
+                quant(c, 0, 2)
             if ok(b):
                 for g in groups(b):
                     stt(mm(b)[:, g * GE : (g + 1) * GE], v4(b)[:, g * GE : (g + 1) * GE], 2.0, t3p_r[g][:])
@@ -280,21 +268,35 @@ def tile_cfkanlayer_kernel(tc, x, cheby_coeffs, bias, out):
                     stt(nh(odd(b, 2), g), nh(q5(b), g), 1.25, t_ps(b, g))
                 for g in groups(b):
                     nc.vector.tensor_tensor(out=nh(odd(b, 3), g), in0=nh(mm(b), g), in1=t_ps(b, g), op=ALU.subtract)
+                for g in groups(b):
+                    nc.scalar.copy(out=slot_g(b, 1, 1, g), in_=t_ps(b, g))
                 affine(nc.gpsimd, slot(b, 0, 1), t3(b).rearrange("p (n h) -> p n h", h=2), 1.0, 0.0)
                 affine(nc.gpsimd, slot(b, 1, 0), z(b).rearrange("p (n h) -> p n h", h=2), 0.5, -1.0)
                 affine(nc.gpsimd, pl_r[b % 2][:, 0, 0, 0 : fd(b)], v4(b), 0.5, -1.0)
             if ok(a):
+                act(v4(a), z(a), ACTF.Square, bias_=-2.0)
+                act(q5(a), z(a), ACTF.Square, bias_=-2.5)
+            if ok(a):
                 for g in groups(a):
                     stt(nh(t3(a), g), nh(z(a), g), 3.0, t_ps(a, g))
             if i == 0:
-                w_rest()
+                for oh in range(2):
+                    w_perm(oh)
+            if i == 1:
+                for m in range(4):
+                    w_copy(nc.vector.tensor_copy, m)
+            if i == 0:
+                ttrans(1)
             if ok(a):
                 t3_to_psum(a)
-            if ok(a + 1):
+            if i > 0 and ok(a + 1):
                 ttrans(a + 1)
+            if i == 0:
+                w_trans()
             if ok(d):
                 outp(d)
+            if i == 2:
+                w_quant()
             if ok(c):
-                quant(c, 1, 2)
                 quant(c, 2, 4)
                 mx(c)

@@ -6,6 +6,7 @@ from concourse.masks import make_identity
 F32 = mybir.dt.float32
 BF16 = mybir.dt.bfloat16
 U32 = mybir.dt.uint32
+I32 = mybir.dt.int32
 U8 = mybir.dt.uint8
 FP8X4 = mybir.dt.float8_e4m3fn_x4
 ALU = mybir.AluOpType
@@ -18,12 +19,13 @@ KD = 8
 D_OUT = 256
 NT = N_TOK // P
 GP = 2
-GE = 2 * GP * P
+DP = 4
+GE = DP * P
 NG = (1,) + (2,) * 15 + (1,)
 NCH = len(NG)
 T0 = [GP * sum(NG[:c]) for c in range(NCH)]
 FD = max(NG) * GE
-PAIRS = ((0, 3), (2, 1), (4, 5), (6, 7))
+NP = KD // 2
 FLOPS = 2 * N_TOK * D_OUT * D_IN * KD
 
 
@@ -41,40 +43,49 @@ def tile_cfkanlayer_kernel(tc, x, cheby_coeffs, bias, out):
                 return [pool.tile(shape, dtype, name="%s_%d" % (name, b)) for b in range(n)]
             return [pool.tile(shape, dtype, name="%s_%d" % (name, b), align_bytes=align) for b in range(n)]
 
-        x_sb = keep.tile([P, NT, D_IN], BF16)
+        x_r = ring(6, [P, 2 * GP, D_IN], BF16, "x")
         w_sb = keep.tile([P, 2, D_IN * KD], BF16)
         b_bf = keep.tile([P, D_OUT], BF16)
-        nc.sync.dma_start(out=x_sb[:, 0:2, :], in_=x_v[:, 0:2, :])
-        nc.sync.dma_start(out=x_sb[:, 2:6, :], in_=x_v[:, 2:6, :])
+
+        def x_load(c):
+            n = GP * NG[c]
+            nc.sync.dma_start(out=x_r[c % 6][:, 0:n, :], in_=x_v[:, T0[c] : T0[c] + n, :])
+
+        x_load(0)
+        x_load(1)
         nc.sync.dma_start(out=w_sb[:], in_=cheby_coeffs.rearrange("(h o) d k -> o h (d k)", h=2))
-        nc.sync.dma_start(out=x_sb[:, 6:14, :], in_=x_v[:, 6:14, :])
+        x_load(2)
+        x_load(3)
         nc.sync.dma_start(out=b_bf[:], in_=bias.rearrange("a o -> (a o)").partition_broadcast(P))
-        for lo, hi in ((14, 30), (30, 64)):
-            nc.sync.dma_start(out=x_sb[:, lo:hi, :], in_=x_v[:, lo:hi, :])
 
         ident = keep.tile([P, P], F32)
         make_identity(nc, ident[:])
 
         tn_r = ring(2, [P, 2 * GP, D_IN], F32, "tn")
-        z_r = ring(2, [P, FD], F32, "z")
-        vw_r = ring(2, [P, 2, FD], F32, "vw")
+        zv_r = ring(2, [P, 2, FD], F32, "zv")
+        w6_r = ring(2, [P, FD], F32, "w6")
         q5_r = ring(2, [P, FD], F32, "q5")
         t3_r = ring(2, [P, FD], F32, "t3")
         mm_r = ring(1, [P, FD], F32, "mm")
-        pl_r = ring(2, [P, 2, 2, FD], BF16, "pl")
-        g01_r = ring(1, [P, 2, 2 * FD], BF16, "g01", align=64)
-        g_r = ring(2, [P, 2, 2 * FD], BF16, "g", align=64)
-        cod_r = ring(2, [P, 4, FD // 2], U32, "cod", align=64)
-        scl_r = ring(2, [P, 4, FD // 2], U8, "scl", align=64)
-        o_r = ring(2, [P, 2 * GP, D_OUT], F32, "o")
-        tp_r = ring(4, [P, 2, GP * P], F32, "tp", pool=ps)
-        acc_r = ring(2, [P, GP, D_OUT], F32, "acc", pool=ps)
-        t3p_r = ring(2, [P, GE], F32, "t3p", pool=ps)
+        pe_r = ring(2, [P, NP - 1, FD], BF16, "pe")
+        p1_r = ring(3, [P, FD], BF16, "p1")
+        mx_r = ring(2, [P, NP, FD], BF16, "mx", align=64)
+        my_r = ring(2, [P, NP, FD], BF16, "my", align=64)
+        sx = keep.tile([P, NP, GE], BF16, align_bytes=64)
+        sy = keep.tile([P, NP, GE], BF16, align_bytes=64)
+        cod_r = ring(2, [P, 2, NP, FD // 4], U32, "cod", align=64)
+        scl_r = ring(2, [P, 2, NP, FD // 4], U8, "scl", align=64)
+        o_r = ring(4, [P, 2 * GP, D_OUT], F32, "o")
+        tp_r = ring(4, [P, DP, P], F32, "tp", pool=ps)
+        acc_r = ring(4, [P, GP, D_OUT], F32, "acc", pool=ps)
+        ones = keep.tile([P, FD], BF16)
         b_f32 = keep.tile([P, D_OUT], F32)
-        w_p = keep.tile([P, 2, KD, D_IN], BF16)
-        w_g = keep.tile([P, 4, 2 * D_OUT], F32, align_bytes=64)
-        w_c = keep.tile([P, 4, D_OUT], U32, align_bytes=64)
-        w_s = keep.tile([P, 4, D_OUT], U8, align_bytes=64)
+        w_p = keep.tile([P, 2, NP, 2, 2 * P], BF16)
+        w_g = keep.tile([P, NP, 2 * D_OUT], F32, align_bytes=64)
+        w_q = keep.tile([P, NP, D_OUT], U32, align_bytes=64)
+        w_qs = keep.tile([P, NP, D_OUT], U8, align_bytes=64)
+        w_c = [keep.tile([P, NP, GP * D_OUT], U32, name="w_c%d" % v, align_bytes=64) for v in range(2)]
+        w_s = [keep.tile([P, NP, GP * D_OUT], U8, name="w_s%d" % v, align_bytes=64) for v in range(2)]
 
         def ok(c):
             return 0 <= c < NCH
@@ -85,17 +96,17 @@ def tile_cfkanlayer_kernel(tc, x, cheby_coeffs, bias, out):
         def fd(c):
             return NG[c] * GE
 
-        def nh(ap, g):
-            return ap[:, g * GE : (g + 1) * GE].rearrange("p (n h) -> p n h", h=2)
+        def ni(ap, g):
+            return ap[:, g * GE : (g + 1) * GE].rearrange("p (n i) -> p n i", i=DP)
 
         def t_ps(c, g):
-            return tp_r[2 * (c % 2) + g][:].rearrange("p h n -> p n h")
+            return tp_r[2 * (c % 2) + g][:].rearrange("p i n -> p n i")
 
         def z(c):
-            return z_r[c % 2][:, 0 : fd(c)]
+            return zv_r[c % 2][:, 0, 0 : fd(c)]
 
         def v4(c):
-            return vw_r[c % 2][:, 0, 0 : fd(c)]
+            return zv_r[c % 2][:, 1, 0 : fd(c)]
 
         def q5(c):
             return q5_r[c % 2][:, 0 : fd(c)]
@@ -104,25 +115,21 @@ def tile_cfkanlayer_kernel(tc, x, cheby_coeffs, bias, out):
             return t3_r[c % 2][:, 0 : fd(c)]
 
         def w6(c):
-            return vw_r[c % 2][:, 1, 0 : fd(c)]
+            return w6_r[c % 2][:, 0 : fd(c)]
 
         def mm(c):
             return mm_r[0][:, 0 : fd(c)]
 
+        def even(c, lo, hi):
+            return pe_r[c % 2][:, lo:hi, 0 : fd(c)]
+
+        def mixed(c, v):
+            if NG[c] == 1:
+                return (sx, sy)[v]
+            return (mx_r, my_r)[v][c % 2]
+
         def odd(c, m):
-            return pl_r[c % 2][:, 1, m - 2, 0 : fd(c)]
-
-        def pair_tile(c, m):
-            return g01_r[0] if m < 2 else g_r[c % 2]
-
-        def grouped(c, m):
-            return pair_tile(c, m)[:, m % 2, 0 : 2 * fd(c)]
-
-        def slot(c, m, s):
-            return grouped(c, m).rearrange("p (n s h) -> p n s h", s=2, h=2)[:, :, s, :]
-
-        def slot_g(c, m, s, g):
-            return slot(c, m, s)[:, g * GP * P : (g + 1) * GP * P]
+            return mixed(c, 1)[:, m, :]
 
         def act(o, i, f, scale=1.0, bias_=0.0):
             nc.scalar.activation(out=o, in_=i, func=f, scale=scale, bias=bias_)
@@ -130,25 +137,16 @@ def tile_cfkanlayer_kernel(tc, x, cheby_coeffs, bias, out):
         def tanh(c):
             for tl in range(GP * NG[c]):
                 act(
-                    tn_r[c % 2][:, tl, :].rearrange("p (c a i) -> p c a i", c=4, a=16, i=4),
-                    x_sb[:, T0[c] + tl, :].rearrange("p (a c i) -> p c a i", c=4, a=16, i=4),
+                    tn_r[c % 2][:, tl, :].rearrange("p (c q e) -> p c q e", c=2, q=16, e=8),
+                    x_r[c % 6][:, tl, :].rearrange("p (q c e) -> p c q e", q=16, c=2, e=8),
                     ACTF.Tanh,
                 )
 
         def ttrans(c):
-            for tl in range(GP * NG[c]):
-                for h in range(2):
-                    nc.tensor.transpose(
-                        tp_r[2 * (c % 2) + tl // GP][:, h, (tl % GP) * P : (tl % GP + 1) * P],
-                        tn_r[c % 2][:, tl, h : D_IN : 2],
-                        ident[:],
-                    )
-
-        def t3_to_psum(c):
             for g in groups(c):
-                nc.tensor.matmul(
-                    t3p_r[g][:], lhsT=ident[:], rhs=t3(c)[:, g * GE : (g + 1) * GE], start=True, stop=True
-                )
+                words = tn_r[c % 2][:, GP * g : GP * (g + 1), :].rearrange("p t d -> p (t d)")
+                for i in range(DP):
+                    nc.tensor.transpose(tp_r[2 * (c % 2) + g][:, i, :], words[:, i : GP * D_IN : DP], ident[:])
 
         def stt(o, a, s, b):
             nc.vector.scalar_tensor_tensor(out=o, in0=a, scalar=s, in1=b, op0=ALU.subtract, op1=ALU.mult)
@@ -156,147 +154,155 @@ def tile_cfkanlayer_kernel(tc, x, cheby_coeffs, bias, out):
         def affine(eng, o, i, s, b):
             eng.tensor_scalar(out=o, in0=i, scalar1=s, scalar2=b, op0=ALU.mult, op1=ALU.add)
 
-        def vector_regroups(c):
-            return c % 2 == 1 and c < NCH - 3
+        def t1(c):
+            return p1_r[c % 3][:, 0 : fd(c)]
 
-        def regroup_s(c):
-            m0 = 1 if vector_regroups(c) else 0
-            nc.scalar.copy(
-                out=g_r[c % 2][:, m0:2, 0 : 2 * fd(c)].bitcast(F32).rearrange("p m (n s) -> p m n s", s=2),
-                in_=pl_r[c % 2][:, :, m0:2, 0 : fd(c)].bitcast(F32).rearrange("p s m n -> p m n s"),
-            )
+        def swap(c):
+            xm, ym = mixed(c, 0), mixed(c, 1)
+            nc.sync.dma_start(out=xm[1:P:2, 0, :], in_=t1(c)[0:P:2])
+            nc.sync.dma_start(out=ym[1:P:2, 0, :], in_=t1(c)[1:P:2])
+            nc.sync.dma_start(out=xm[1:P:2, 1:NP, :], in_=ym[0:P:2, 1:NP, :])
+            nc.sync.dma_start(out=xm[0:P:2, 1:NP, :], in_=even(c, 0, NP - 1)[0:P:2])
 
-        def regroup_v(c):
-            nc.vector.tensor_copy(
-                out=grouped(c, 2).rearrange("p (n s e) -> p n s e", s=2, e=2),
-                in_=pl_r[c % 2][:, :, 0, 0 : fd(c)].rearrange("p s (n e) -> p n s e", e=2),
-            )
+        def swap_rest(c):
+            nc.sync.dma_start(out=mixed(c, 1)[0:P:2, 1:NP, :], in_=even(c, 0, NP - 1)[1:P:2])
 
-        def quant(c, m0, m1):
-            if NG[c] < max(NG) and m1 - m0 > 1:
-                for m in range(m0, m1):
-                    quant(c, m, m + 1)
-                return
-            n = fd(c) // 2
+        def quant(c, v):
+            n = fd(c) // 4
+            codes = cod_r[c % 2][:, v].rearrange("p m n -> p (m n)")[:, 0 : NP * n]
+            scales = scl_r[c % 2][:, v].rearrange("p m n -> p (m n)")[:, 0 : NP * n]
             nc.vector.quantize_mx(
-                out=cod_r[c % 2][:, m0:m1, 0:n].rearrange("p m n -> p (m n)").bitcast(FP8X4),
-                scales=scl_r[c % 2][:, m0:m1, 0:n].rearrange("p m n -> p (m n)"),
-                in_=grouped(c, m0) if m1 - m0 == 1 else pair_tile(c, m0)[:].rearrange("p m f -> p (m f)"),
+                out=codes.bitcast(FP8X4), scales=scales, in_=mixed(c, v)[:].rearrange("p m f -> p (m f)")
             )
 
         def mx(c):
-            for g in groups(c):
-                for j in range(GP):
-                    cols = slice((GP * g + j) * P, (GP * g + j + 1) * P)
-                    for m in range(4):
+            n = fd(c) // 4
+            for v in range(2):
+                for g in groups(c):
+                    for m in range(NP):
+                        cols = slice(m * n + g * P, m * n + (g + 1) * P)
                         nc.tensor.matmul_mx(
-                            out=acc_r[g][:, j, :],
-                            lhsT=cod_r[c % 2][:, m, cols].bitcast(FP8X4),
-                            lhsT_scale=scl_r[c % 2][:, m, cols],
-                            rhs=w_c[:, m, :].bitcast(FP8X4),
-                            rhs_scale=w_s[:, m, :],
-                            start=(m == 0),
-                            stop=(m == 3),
+                            out=acc_r[2 * (c % 2) + g][:].rearrange("p t o -> p (t o)"),
+                            lhsT=cod_r[c % 2][:, v].rearrange("p m n -> p (m n)")[:, cols].bitcast(FP8X4),
+                            lhsT_scale=scl_r[c % 2][:, v].rearrange("p m n -> p (m n)")[:, cols],
+                            rhs=w_c[v][:, m, :].bitcast(FP8X4),
+                            rhs_scale=w_s[v][:, m, :],
+                            start=(m == 0 and v == 0),
+                            stop=(m == NP - 1 and v == 1),
                         )
 
         def outp(c):
             for g in groups(c):
                 nc.vector.tensor_tensor(
-                    out=o_r[c % 2][:, GP * g : GP * (g + 1), :],
-                    in0=acc_r[g][:],
+                    out=o_r[c % 4][:, GP * g : GP * (g + 1), :],
+                    in0=acc_r[2 * (c % 2) + g][:],
                     in1=b_f32[:].unsqueeze(1).to_broadcast([P, GP, D_OUT]),
                     op=ALU.add,
                 )
             nt = GP * NG[c]
-            nc.sync.dma_start(out=out_v[:, T0[c] : T0[c] + nt, :], in_=o_r[c % 2][:, 0:nt, :])
+            nc.sync.dma_start(out=out_v[:, T0[c] : T0[c] + nt, :], in_=o_r[c % 4][:, 0:nt, :])
 
-        def w_perm(oh):
-            nc.vector.tensor_copy(
-                out=w_p[:, oh].rearrange("o k (c a i) -> o k c a i", c=4, a=16, i=4),
-                in_=w_sb[:, oh, :].rearrange("o (a c i k) -> o k c a i", a=16, c=4, i=4, k=KD),
-            )
-
-        w_t = (acc_r[0], acc_r[1], t3p_r[1], tp_r[1])
-
-        def w_words(m):
-            return t3p_r[1][:].rearrange("p (s o) -> p s o", s=2) if m == 2 else w_t[m][:]
-
-        def w_trans():
-            for m in range(4):
-                for s in range(2):
-                    for oh in range(2):
-                        nc.tensor.transpose(
-                            w_words(m)[:, s, oh * P : (oh + 1) * P], w_p[:, oh, PAIRS[m][s], :].bitcast(F32), ident[:]
+        def w_perm(oh, copy):
+            src = w_sb[:, oh, :].rearrange("o (q c v h e j s) -> o c v h j q s e", q=16, c=2, v=2, h=2, e=2, j=NP, s=2)
+            for v in range(2):
+                for h in range(2):
+                    for c in range(2):
+                        lo = 2 * (64 * v + 32 * c)
+                        copy(
+                            out=w_p[:, oh, :, h, lo : lo + 64].rearrange("o j (q s e) -> o j q s e", q=16, s=2, e=2),
+                            in_=src[:, c, v, h],
                         )
 
-        def w_copy(copy, m):
-            copy(out=w_g[:, m, :].rearrange("p (o s) -> p o s", s=2), in_=w_words(m).rearrange("p s o -> p o s"))
+        def w_trans():
+            for m in range(NP):
+                for h in range(2):
+                    for oh in range(2):
+                        nc.tensor.transpose(
+                            acc_r[m][:, h, oh * P : (oh + 1) * P], w_p[:, oh, m, h, :].bitcast(F32), ident[:]
+                        )
+
+        def w_copy(m):
+            nc.vector.tensor_copy(
+                out=w_g[:, m, :].rearrange("p (o h) -> p o h", h=2), in_=acc_r[m][:].rearrange("p h o -> p o h")
+            )
 
         def w_quant():
             nc.vector.quantize_mx(
-                out=w_c[:].rearrange("p m o -> p (m o)").bitcast(FP8X4),
-                scales=w_s[:].rearrange("p m o -> p (m o)"),
+                out=w_q[:].rearrange("p m o -> p (m o)").bitcast(FP8X4),
+                scales=w_qs[:].rearrange("p m o -> p (m o)"),
                 in_=w_g[:].rearrange("p m f -> p (m f)").bitcast(BF16),
             )
+            for v in range(2):
+                for t in range(GP):
+                    rows, src = slice(64 * t, 64 * t + 64), slice(64 * v, 64 * v + 64)
+                    cols = slice(t * D_OUT, (t + 1) * D_OUT)
+                    nc.sync.dma_start(out=w_c[v][rows, :, cols].bitcast(I32), in_=w_q[src].bitcast(I32))
+                    nc.sync.dma_start(out=w_s[v][rows, :, cols].bitcast(I32), in_=w_qs[src].bitcast(I32))
 
         tanh(0)
         ttrans(0)
-        nc.vector.memset(g01_r[0][:, 0, :], 1.0)
+        nc.vector.memset(ones[:], 1.0)
+        nc.vector.memset(w_qs[:].bitcast(I32), 0)
+        for v in range(2):
+            nc.gpsimd.memset(w_c[v][:].bitcast(I32), 0)
+            nc.gpsimd.memset(w_s[v][:].bitcast(I32), 0)
+        nc.sync.dma_start(out=sx[:, 0, :], in_=ones[:, 0:GE])
+        nc.sync.dma_start(out=sy[:, 0, :], in_=ones[:, 0:GE])
+        for b in range(2):
+            nc.sync.dma_start(out=mx_r[b][:, 0, :], in_=ones[:])
+            nc.sync.dma_start(out=my_r[b][:, 0, :], in_=ones[:])
         nc.gpsimd.tensor_copy(out=b_f32[:], in_=b_bf[:])
 
         for i in range(NCH + 3):
             a, b, c, d = i, i - 1, i - 2, i - 3
-            if ok(c):
-                affine(nc.vector, pl_r[c % 2][:, 0, 1, 0 : fd(c)], w6(c), 0.5, -1.0)
             if ok(a):
                 for g in groups(a):
-                    act(nh(z(a), g), t_ps(a, g), ACTF.Square, scale=2.0)
+                    act(ni(z(a), g), t_ps(a, g), ACTF.Square, scale=2.0)
+                for g in groups(a):
+                    nc.scalar.copy(out=ni(t1(a), g), in_=t_ps(a, g))
             if ok(b):
                 act(w6(b), t3(b), ACTF.Square, scale=2.0)
-            if ok(c):
-                regroup_s(c)
+                act(even(b, 2, 3)[:, 0, :], w6(b), ACTF.Identity, scale=0.5, bias_=-1.0)
+            if ok(b):
+                stt(mm(b), v4(b), 2.0, t3(b))
+                affine(nc.gpsimd, odd(b, 1)[:, 0 : fd(b)], t3(b), 1.0, 0.0)
+                affine(nc.gpsimd, even(b, 0, 2), zv_r[b % 2][:, :, 0 : fd(b)], 0.5, -1.0)
+                for g in groups(b):
+                    stt(ni(odd(b, 2), g), ni(q5(b), g), 1.25, t_ps(b, g))
+                for g in groups(b):
+                    nc.vector.tensor_tensor(out=ni(odd(b, 3), g), in0=ni(mm(b), g), in1=t_ps(b, g), op=ALU.subtract)
+                swap(b)
+                if b >= NCH - 2:
+                    swap_rest(b)
             if ok(a + 1):
                 tanh(a + 1)
-            if ok(c):
-                if vector_regroups(c):
-                    regroup_v(c)
-                quant(c, 0, 2)
-            if ok(b):
-                for g in groups(b):
-                    stt(mm(b)[:, g * GE : (g + 1) * GE], v4(b)[:, g * GE : (g + 1) * GE], 2.0, t3p_r[g][:])
-                for g in groups(b):
-                    stt(nh(odd(b, 2), g), nh(q5(b), g), 1.25, t_ps(b, g))
-                for g in groups(b):
-                    nc.vector.tensor_tensor(out=nh(odd(b, 3), g), in0=nh(mm(b), g), in1=t_ps(b, g), op=ALU.subtract)
-                for g in groups(b):
-                    nc.scalar.copy(out=slot_g(b, 1, 1, g), in_=t_ps(b, g))
-                affine(nc.gpsimd, slot(b, 0, 1), t3(b).rearrange("p (n h) -> p n h", h=2), 1.0, 0.0)
-                affine(nc.gpsimd, slot(b, 1, 0), z(b).rearrange("p (n h) -> p n h", h=2), 0.5, -1.0)
-                affine(nc.gpsimd, pl_r[b % 2][:, 0, 0, 0 : fd(b)], v4(b), 0.5, -1.0)
             if ok(a):
                 act(v4(a), z(a), ACTF.Square, bias_=-2.0)
                 act(q5(a), z(a), ACTF.Square, bias_=-2.5)
             if ok(a):
                 for g in groups(a):
-                    stt(nh(t3(a), g), nh(z(a), g), 3.0, t_ps(a, g))
+                    stt(ni(t3(a), g), ni(z(a), g), 3.0, t_ps(a, g))
             if i == 0:
-                for oh in range(2):
-                    w_perm(oh)
+                w_perm(0, nc.vector.tensor_copy)
+                w_perm(1, nc.scalar.copy)
             if i == 1:
-                for m in range(4):
-                    w_copy(nc.vector.tensor_copy, m)
-            if i == 0:
-                ttrans(1)
-            if ok(a):
-                t3_to_psum(a)
-            if i > 0 and ok(a + 1):
+                for m in range(NP):
+                    w_copy(m)
+                w_quant()
+            if ok(a + 1):
                 ttrans(a + 1)
             if i == 0:
                 w_trans()
-            if ok(d):
+            if ok(a + 4):
+                x_load(a + 4)
+            if ok(d) and c < NCH - 2:
                 outp(d)
-            if i == 2:
-                w_quant()
             if ok(c):
-                quant(c, 2, 4)
+                for v in range(2):
+                    quant(c, v)
+            if ok(d) and c >= NCH - 2:
+                outp(d)
+            if ok(b) and b < NCH - 2:
+                swap_rest(b)
+            if ok(c):
                 mx(c)

@@ -73,6 +73,7 @@ def tile_cfkanlayer_kernel(tc, x, cheby_coeffs, bias, out):
         my_r = ring(2, [P, NP, FD], BF16, "my", align=64)
         sx = keep.tile([P, NP, GE], BF16, align_bytes=64)
         sy = keep.tile([P, NP, GE], BF16, align_bytes=64)
+        so = keep.tile([P, NP, GE], BF16)
         cod_r = ring(2, [P, 2, NP, FD // 4], U32, "cod", align=64)
         scl_r = ring(2, [P, 2, NP, FD // 4], U8, "scl", align=64)
         o_r = ring(4, [P, 2 * GP, D_OUT], F32, "o")
@@ -128,8 +129,11 @@ def tile_cfkanlayer_kernel(tc, x, cheby_coeffs, bias, out):
                 return (sx, sy)[v]
             return (mx_r, my_r)[v][c % 2]
 
+        def odds(c):
+            return so if NG[c] == 1 else mixed(c, 1)
+
         def odd(c, m):
-            return mixed(c, 1)[:, m, :]
+            return odds(c)[:, m, :]
 
         def act(o, i, f, scale=1.0, bias_=0.0):
             nc.scalar.activation(out=o, in_=i, func=f, scale=scale, bias=bias_)
@@ -161,7 +165,9 @@ def tile_cfkanlayer_kernel(tc, x, cheby_coeffs, bias, out):
             xm, ym = mixed(c, 0), mixed(c, 1)
             nc.sync.dma_start(out=xm[1:P:2, 0, :], in_=t1(c)[0:P:2])
             nc.sync.dma_start(out=ym[1:P:2, 0, :], in_=t1(c)[1:P:2])
-            nc.sync.dma_start(out=xm[1:P:2, 1:NP, :], in_=ym[0:P:2, 1:NP, :])
+            nc.sync.dma_start(out=xm[1:P:2, 1:NP, :], in_=odds(c)[0:P:2, 1:NP, :])
+            if NG[c] == 1:
+                nc.sync.dma_start(out=ym[1:P:2, 1:NP, :], in_=so[1:P:2, 1:NP, :])
             nc.sync.dma_start(out=xm[0:P:2, 1:NP, :], in_=even(c, 0, NP - 1)[0:P:2])
 
         def swap_rest(c):
@@ -258,8 +264,6 @@ def tile_cfkanlayer_kernel(tc, x, cheby_coeffs, bias, out):
             if ok(a):
                 for g in groups(a):
                     act(ni(z(a), g), t_ps(a, g), ACTF.Square, scale=2.0)
-                for g in groups(a):
-                    nc.scalar.copy(out=ni(t1(a), g), in_=t_ps(a, g))
             if ok(b):
                 act(w6(b), t3(b), ACTF.Square, scale=2.0)
                 act(even(b, 2, 3)[:, 0, :], w6(b), ACTF.Identity, scale=0.5, bias_=-1.0)
@@ -272,16 +276,17 @@ def tile_cfkanlayer_kernel(tc, x, cheby_coeffs, bias, out):
                 for g in groups(b):
                     nc.vector.tensor_tensor(out=ni(odd(b, 3), g), in0=ni(mm(b), g), in1=t_ps(b, g), op=ALU.subtract)
                 swap(b)
-                if b >= NCH - 2:
+                if b == 0 or b >= NCH - 2:
                     swap_rest(b)
             if ok(a + 1):
                 tanh(a + 1)
             if ok(a):
-                act(v4(a), z(a), ACTF.Square, bias_=-2.0)
-                act(q5(a), z(a), ACTF.Square, bias_=-2.5)
-            if ok(a):
                 for g in groups(a):
                     stt(ni(t3(a), g), ni(z(a), g), 3.0, t_ps(a, g))
+                act(v4(a), z(a), ACTF.Square, bias_=-2.0)
+                act(q5(a), z(a), ACTF.Square, bias_=-2.5)
+                for g in groups(a):
+                    nc.scalar.copy(out=ni(t1(a), g), in_=t_ps(a, g))
             if i == 0:
                 w_perm(0, nc.vector.tensor_copy)
                 w_perm(1, nc.scalar.copy)
@@ -302,7 +307,7 @@ def tile_cfkanlayer_kernel(tc, x, cheby_coeffs, bias, out):
                     quant(c, v)
             if ok(d) and c >= NCH - 2:
                 outp(d)
-            if ok(b) and b < NCH - 2:
+            if 0 < b < NCH - 2:
                 swap_rest(b)
             if ok(c):
                 mx(c)

@@ -53,7 +53,9 @@ def tile_cfkanlayer_kernel(tc, x, cheby_coeffs, bias, out):
 
         x_load(0)
         x_load(1)
-        nc.sync.dma_start(out=w_sb[:], in_=cheby_coeffs.rearrange("(h o) d k -> o h (d k)", h=2))
+        w_v = cheby_coeffs.rearrange("(h o) d k -> o h (d k)", h=2)
+        for oh in range(2):
+            nc.sync.dma_start(out=w_sb[:, oh, :], in_=w_v[:, oh, :])
         x_load(2)
         x_load(3)
         nc.sync.dma_start(out=b_bf[:], in_=bias.rearrange("a o -> (a o)").partition_broadcast(P))
@@ -62,12 +64,12 @@ def tile_cfkanlayer_kernel(tc, x, cheby_coeffs, bias, out):
         make_identity(nc, ident[:])
 
         tn_r = ring(2, [P, 2 * GP, D_IN], F32, "tn")
-        zv_r = ring(2, [P, 2, FD], F32, "zv")
+        zv_r = ring(3, [P, 2, FD], F32, "zv")
         w6_r = ring(2, [P, FD], F32, "w6")
-        q5_r = ring(2, [P, FD], F32, "q5")
+        q5_r = ring(3, [P, FD], F32, "q5")
         t3_r = ring(2, [P, FD], F32, "t3")
         mm_r = ring(1, [P, FD], F32, "mm")
-        pe_r = ring(2, [P, NP - 1, FD], BF16, "pe")
+        pe_r = ring(3, [P, NP - 1, FD], BF16, "pe")
         p1_r = ring(3, [P, FD], BF16, "p1")
         mx_r = ring(2, [P, NP, FD], BF16, "mx", align=64)
         my_r = ring(2, [P, NP, FD], BF16, "my", align=64)
@@ -104,13 +106,13 @@ def tile_cfkanlayer_kernel(tc, x, cheby_coeffs, bias, out):
             return tp_r[2 * (c % 2) + g][:].rearrange("p i n -> p n i")
 
         def z(c):
-            return zv_r[c % 2][:, 0, 0 : fd(c)]
+            return zv_r[c % 3][:, 0, 0 : fd(c)]
 
         def v4(c):
-            return zv_r[c % 2][:, 1, 0 : fd(c)]
+            return zv_r[c % 3][:, 1, 0 : fd(c)]
 
         def q5(c):
-            return q5_r[c % 2][:, 0 : fd(c)]
+            return q5_r[c % 3][:, 0 : fd(c)]
 
         def t3(c):
             return t3_r[c % 2][:, 0 : fd(c)]
@@ -122,7 +124,7 @@ def tile_cfkanlayer_kernel(tc, x, cheby_coeffs, bias, out):
             return mm_r[0][:, 0 : fd(c)]
 
         def even(c, lo, hi):
-            return pe_r[c % 2][:, lo:hi, 0 : fd(c)]
+            return pe_r[c % 3][:, lo:hi, 0 : fd(c)]
 
         def mixed(c, v):
             if NG[c] == 1:
@@ -270,7 +272,7 @@ def tile_cfkanlayer_kernel(tc, x, cheby_coeffs, bias, out):
             if ok(b):
                 stt(mm(b), v4(b), 2.0, t3(b))
                 affine(nc.gpsimd, odd(b, 1)[:, 0 : fd(b)], t3(b), 1.0, 0.0)
-                affine(nc.gpsimd, even(b, 0, 2), zv_r[b % 2][:, :, 0 : fd(b)], 0.5, -1.0)
+                affine(nc.gpsimd, even(b, 0, 2), zv_r[b % 3][:, :, 0 : fd(b)], 0.5, -1.0)
                 for g in groups(b):
                     stt(ni(odd(b, 2), g), ni(q5(b), g), 1.25, t_ps(b, g))
                 for g in groups(b):

@@ -82,6 +82,7 @@ def tile_cfkanlayer_kernel(tc, x, cheby_coeffs, bias, out):
         tp_r = ring(4, [P, DP, P], F32, "tp", pool=ps)
         acc_r = ring(4, [P, GP, D_OUT], F32, "acc", pool=ps)
         ones = keep.tile([P, FD], BF16)
+        trig = keep.tile([P, 1], F32)
         b_f32 = keep.tile([P, D_OUT], F32)
         w_p = keep.tile([P, 2, NP, 2, 2 * P], BF16)
         w_g = keep.tile([P, NP, 2 * D_OUT], F32, align_bytes=64)
@@ -160,6 +161,9 @@ def tile_cfkanlayer_kernel(tc, x, cheby_coeffs, bias, out):
         def affine(eng, o, i, s, b):
             eng.tensor_scalar(out=o, in0=i, scalar1=s, scalar2=b, op0=ALU.mult, op1=ALU.add)
 
+        def gp_copy(out, in_):
+            affine(nc.gpsimd, out, in_, 1.0, 0.0)
+
         def t1(c):
             return p1_r[c % 3][:, 0 : fd(c)]
 
@@ -211,13 +215,13 @@ def tile_cfkanlayer_kernel(tc, x, cheby_coeffs, bias, out):
             nc.sync.dma_start(out=out_v[:, T0[c] : T0[c] + nt, :], in_=o_r[c % 4][:, 0:nt, :])
 
         def w_perm(oh, copy):
-            src = w_sb[:, oh, :].rearrange("o (q c v h e j s) -> o c v h j q s e", q=16, c=2, v=2, h=2, e=2, j=NP, s=2)
+            src = w_sb[:, oh, :].rearrange("o (q c v h e j s) -> o c v h q j s e", q=16, c=2, v=2, h=2, e=2, j=NP, s=2)
             for v in range(2):
                 for h in range(2):
                     for c in range(2):
                         lo = 2 * (64 * v + 32 * c)
                         copy(
-                            out=w_p[:, oh, :, h, lo : lo + 64].rearrange("o j (q s e) -> o j q s e", q=16, s=2, e=2),
+                            out=w_p[:, oh, :, h, lo : lo + 64].rearrange("o j (q s e) -> o q j s e", q=16, s=2, e=2),
                             in_=src[:, c, v, h],
                         )
 
@@ -252,14 +256,13 @@ def tile_cfkanlayer_kernel(tc, x, cheby_coeffs, bias, out):
         nc.vector.memset(ones[:], 1.0)
         nc.vector.memset(w_qs[:].bitcast(I32), 0)
         for v in range(2):
-            nc.gpsimd.memset(w_c[v][:].bitcast(I32), 0)
-            nc.gpsimd.memset(w_s[v][:].bitcast(I32), 0)
+            nc.vector.memset(w_c[v][:].bitcast(I32), 0)
+            nc.vector.memset(w_s[v][:].bitcast(I32), 0)
         nc.sync.dma_start(out=sx[:, 0, :], in_=ones[:, 0:GE])
         nc.sync.dma_start(out=sy[:, 0, :], in_=ones[:, 0:GE])
         for b in range(2):
             nc.sync.dma_start(out=mx_r[b][:, 0, :], in_=ones[:])
             nc.sync.dma_start(out=my_r[b][:, 0, :], in_=ones[:])
-        nc.gpsimd.tensor_copy(out=b_f32[:], in_=b_bf[:])
 
         for i in range(NCH + 3):
             a, b, c, d = i, i - 1, i - 2, i - 3
@@ -271,6 +274,7 @@ def tile_cfkanlayer_kernel(tc, x, cheby_coeffs, bias, out):
                 act(even(b, 2, 3)[:, 0, :], w6(b), ACTF.Identity, scale=0.5, bias_=-1.0)
             if ok(b):
                 stt(mm(b), v4(b), 2.0, t3(b))
+                affine(nc.gpsimd, trig[:], mm(b)[:, fd(b) - 1 : fd(b)], 1.0, 0.0)
                 affine(nc.gpsimd, odd(b, 1)[:, 0 : fd(b)], t3(b), 1.0, 0.0)
                 affine(nc.gpsimd, even(b, 0, 2), zv_r[b % 3][:, :, 0 : fd(b)], 0.5, -1.0)
                 for g in groups(b):
@@ -290,9 +294,10 @@ def tile_cfkanlayer_kernel(tc, x, cheby_coeffs, bias, out):
                 for g in groups(a):
                     nc.scalar.copy(out=ni(t1(a), g), in_=t_ps(a, g))
             if i == 0:
-                w_perm(0, nc.vector.tensor_copy)
-                w_perm(1, nc.scalar.copy)
+                w_perm(0, gp_copy)
+                w_perm(1, gp_copy)
             if i == 1:
+                gp_copy(out=b_f32[:], in_=b_bf[:])
                 for m in range(NP):
                     w_copy(m)
                 w_quant()

@@ -161,9 +161,6 @@ def tile_cfkanlayer_kernel(tc, x, cheby_coeffs, bias, out):
         def affine(eng, o, i, s, b):
             eng.tensor_scalar(out=o, in0=i, scalar1=s, scalar2=b, op0=ALU.mult, op1=ALU.add)
 
-        def gp_copy(out, in_):
-            affine(nc.gpsimd, out, in_, 1.0, 0.0)
-
         def t1(c):
             return p1_r[c % 3][:, 0 : fd(c)]
 
@@ -215,13 +212,13 @@ def tile_cfkanlayer_kernel(tc, x, cheby_coeffs, bias, out):
             nc.sync.dma_start(out=out_v[:, T0[c] : T0[c] + nt, :], in_=o_r[c % 4][:, 0:nt, :])
 
         def w_perm(oh, copy):
-            src = w_sb[:, oh, :].rearrange("o (q c v h e j s) -> o c v h q j s e", q=16, c=2, v=2, h=2, e=2, j=NP, s=2)
+            src = w_sb[:, oh, :].rearrange("o (q c v h e j s) -> o c v h j q s e", q=16, c=2, v=2, h=2, e=2, j=NP, s=2)
             for v in range(2):
                 for h in range(2):
                     for c in range(2):
                         lo = 2 * (64 * v + 32 * c)
                         copy(
-                            out=w_p[:, oh, :, h, lo : lo + 64].rearrange("o j (q s e) -> o q j s e", q=16, s=2, e=2),
+                            out=w_p[:, oh, :, h, lo : lo + 64].rearrange("o j (q s e) -> o j q s e", q=16, s=2, e=2),
                             in_=src[:, c, v, h],
                         )
 
@@ -274,9 +271,13 @@ def tile_cfkanlayer_kernel(tc, x, cheby_coeffs, bias, out):
                 act(even(b, 2, 3)[:, 0, :], w6(b), ACTF.Identity, scale=0.5, bias_=-1.0)
             if ok(b):
                 stt(mm(b), v4(b), 2.0, t3(b))
-                affine(nc.gpsimd, trig[:], mm(b)[:, fd(b) - 1 : fd(b)], 1.0, 0.0)
-                affine(nc.gpsimd, odd(b, 1)[:, 0 : fd(b)], t3(b), 1.0, 0.0)
-                affine(nc.gpsimd, even(b, 0, 2), zv_r[b % 3][:, :, 0 : fd(b)], 0.5, -1.0)
+                if b == NCH - 1:
+                    act(odd(b, 1), t3(b), ACTF.Identity)
+                    act(even(b, 0, 2), zv_r[b % 3][:, :, 0 : fd(b)], ACTF.Identity, scale=0.5, bias_=-1.0)
+                else:
+                    affine(nc.gpsimd, trig[:], mm(b)[:, fd(b) - 1 : fd(b)], 1.0, 0.0)
+                    affine(nc.gpsimd, odd(b, 1)[:, 0 : fd(b)], t3(b), 1.0, 0.0)
+                    affine(nc.gpsimd, even(b, 0, 2), zv_r[b % 3][:, :, 0 : fd(b)], 0.5, -1.0)
                 for g in groups(b):
                     stt(ni(odd(b, 2), g), ni(q5(b), g), 1.25, t_ps(b, g))
                 for g in groups(b):
@@ -294,10 +295,10 @@ def tile_cfkanlayer_kernel(tc, x, cheby_coeffs, bias, out):
                 for g in groups(a):
                     nc.scalar.copy(out=ni(t1(a), g), in_=t_ps(a, g))
             if i == 0:
-                w_perm(0, gp_copy)
-                w_perm(1, gp_copy)
+                w_perm(0, nc.vector.tensor_copy)
+                w_perm(1, nc.scalar.copy)
             if i == 1:
-                gp_copy(out=b_f32[:], in_=b_bf[:])
+                affine(nc.gpsimd, b_f32[:], b_bf[:], 1.0, 0.0)
                 for m in range(NP):
                     w_copy(m)
                 w_quant()

@@ -262,7 +262,7 @@ def tile_cfkanlayer_kernel(tc, x, cheby_coeffs, bias, out):
             nc.sync.dma_start(out=my_r[b][:, 0, :], in_=ones[:])
 
         for i in range(NCH + 3):
-            a, b, c, d = i, i - 1, i - 2, i - 3
+            a, b, c, d, e = i, i - 1, i - 2, i - 3, i - 4
             if ok(a):
                 for g in groups(a):
                     act(ni(z(a), g), t_ps(a, g), ACTF.Square, scale=2.0)
@@ -308,12 +308,14 @@ def tile_cfkanlayer_kernel(tc, x, cheby_coeffs, bias, out):
                 w_trans()
             if ok(a + 4):
                 x_load(a + 4)
-            if ok(d) and c < NCH - 2:
-                outp(d)
+            if 0 <= e < NCH - 3:
+                outp(e)
             if ok(c):
                 for v in range(2):
                     quant(c, v)
-            if ok(d) and c >= NCH - 2:
+            if d == NCH - 3:
+                outp(e + 1)
+            if ok(d) and c >= NCH - 1:
                 outp(d)
             if 0 < b < NCH - 2:
                 swap_rest(b)

@@ -250,6 +250,7 @@ def tile_cfkanlayer_kernel(tc, x, cheby_coeffs, bias, out):
 
         tanh(0)
         ttrans(0)
+        tanh(1)
         nc.vector.memset(ones[:], 1.0)
         nc.vector.memset(w_qs[:].bitcast(I32), 0)
         for v in range(2):
@@ -268,16 +269,20 @@ def tile_cfkanlayer_kernel(tc, x, cheby_coeffs, bias, out):
                     act(ni(z(a), g), t_ps(a, g), ACTF.Square, scale=2.0)
             if ok(b):
                 act(w6(b), t3(b), ACTF.Square, scale=2.0)
-                act(even(b, 2, 3)[:, 0, :], w6(b), ACTF.Identity, scale=0.5, bias_=-1.0)
+                if b >= 2:
+                    act(even(b, 2, 3)[:, 0, :], w6(b), ACTF.Identity, scale=0.5, bias_=-1.0)
             if ok(b):
                 stt(mm(b), v4(b), 2.0, t3(b))
                 if b == NCH - 1:
                     act(odd(b, 1), t3(b), ACTF.Identity)
                     act(even(b, 0, 2), zv_r[b % 3][:, :, 0 : fd(b)], ACTF.Identity, scale=0.5, bias_=-1.0)
                 else:
-                    affine(nc.gpsimd, trig[:], mm(b)[:, fd(b) - 1 : fd(b)], 1.0, 0.0)
+                    if b < 4:
+                        affine(nc.gpsimd, trig[:], mm(b)[:, fd(b) - 1 : fd(b)], 1.0, 0.0)
                     affine(nc.gpsimd, odd(b, 1)[:, 0 : fd(b)], t3(b), 1.0, 0.0)
                     affine(nc.gpsimd, even(b, 0, 2), zv_r[b % 3][:, :, 0 : fd(b)], 0.5, -1.0)
+                    if b < 2:
+                        affine(nc.gpsimd, even(b, 2, 3)[:, 0, :], w6(b), 0.5, -1.0)
                 for g in groups(b):
                     stt(ni(odd(b, 2), g), ni(q5(b), g), 1.25, t_ps(b, g))
                 for g in groups(b):
@@ -285,7 +290,7 @@ def tile_cfkanlayer_kernel(tc, x, cheby_coeffs, bias, out):
                 swap(b)
                 if b == 0 or b >= NCH - 2:
                     swap_rest(b)
-            if ok(a + 1):
+            if 0 < a and ok(a + 1):
                 tanh(a + 1)
             if ok(a):
                 for g in groups(a):

@@ -6,7 +6,6 @@ from concourse.masks import make_identity
 F32 = mybir.dt.float32
 BF16 = mybir.dt.bfloat16
 U32 = mybir.dt.uint32
-I32 = mybir.dt.int32
 U8 = mybir.dt.uint8
 FP8X4 = mybir.dt.float8_e4m3fn_x4
 ALU = mybir.AluOpType
@@ -63,7 +62,7 @@ def tile_cfkanlayer_kernel(tc, x, cheby_coeffs, bias, out):
         ident = keep.tile([P, P], F32)
         make_identity(nc, ident[:])
 
-        tn_r = ring(2, [P, 2 * GP, D_IN], F32, "tn")
+        tn_r = ring(2, [P, 2, GE], F32, "tn")
         zv_r = ring(3, [P, 2, FD], F32, "zv")
         w6_r = ring(2, [P, FD], F32, "w6")
         q5_r = ring(3, [P, FD], F32, "q5")
@@ -88,8 +87,6 @@ def tile_cfkanlayer_kernel(tc, x, cheby_coeffs, bias, out):
         w_g = keep.tile([P, NP, 2 * D_OUT], F32, align_bytes=64)
         w_q = keep.tile([P, NP, D_OUT], U32, align_bytes=64)
         w_qs = keep.tile([P, NP, D_OUT], U8, align_bytes=64)
-        w_c = [keep.tile([P, NP, GP * D_OUT], U32, name="w_c%d" % v, align_bytes=64) for v in range(2)]
-        w_s = [keep.tile([P, NP, GP * D_OUT], U8, name="w_s%d" % v, align_bytes=64) for v in range(2)]
 
         def ok(c):
             return 0 <= c < NCH
@@ -144,16 +141,16 @@ def tile_cfkanlayer_kernel(tc, x, cheby_coeffs, bias, out):
         def tanh(c):
             for tl in range(GP * NG[c]):
                 act(
-                    tn_r[c % 2][:, tl, :].rearrange("p (c q e) -> p c q e", c=2, q=16, e=8),
-                    x_r[c % 6][:, tl, :].rearrange("p (q c e) -> p c q e", q=16, c=2, e=8),
+                    tn_r[c % 2][:, tl // GP, :].rearrange("p (r e t j) -> p t r e j", r=4, e=16, t=GP)[:, tl % GP],
+                    x_r[c % 6][:, tl, :].rearrange("p (r j e) -> p r e j", r=4, j=DP),
                     ACTF.Tanh,
                 )
 
         def ttrans(c):
             for g in groups(c):
-                words = tn_r[c % 2][:, GP * g : GP * (g + 1), :].rearrange("p t d -> p (t d)")
+                words = tn_r[c % 2][:, g, :]
                 for i in range(DP):
-                    nc.tensor.transpose(tp_r[2 * (c % 2) + g][:, i, :], words[:, i : GP * D_IN : DP], ident[:])
+                    nc.tensor.transpose(tp_r[2 * (c % 2) + g][:, i, :], words[:, i : GE : DP], ident[:])
 
         def stt(o, a, s, b):
             nc.vector.scalar_tensor_tensor(out=o, in0=a, scalar=s, in1=b, op0=ALU.subtract, op1=ALU.mult)
@@ -191,13 +188,13 @@ def tile_cfkanlayer_kernel(tc, x, cheby_coeffs, bias, out):
                     for m in range(NP):
                         cols = slice(m * n + g * P, m * n + (g + 1) * P)
                         nc.tensor.matmul_mx(
-                            out=acc_r[2 * (c % 2) + g][:].rearrange("p t o -> p (t o)"),
+                            out=acc_r[2 * (c % 2) + g][:, v, :],
                             lhsT=cod_r[c % 2][:, v].rearrange("p m n -> p (m n)")[:, cols].bitcast(FP8X4),
                             lhsT_scale=scl_r[c % 2][:, v].rearrange("p m n -> p (m n)")[:, cols],
-                            rhs=w_c[v][:, m, :].bitcast(FP8X4),
-                            rhs_scale=w_s[v][:, m, :],
-                            start=(m == 0 and v == 0),
-                            stop=(m == NP - 1 and v == 1),
+                            rhs=w_q[:, m, :].bitcast(FP8X4),
+                            rhs_scale=w_qs[:, m, :],
+                            start=(m == 0),
+                            stop=(m == NP - 1),
                         )
 
         def outp(c):
@@ -212,15 +209,13 @@ def tile_cfkanlayer_kernel(tc, x, cheby_coeffs, bias, out):
             nc.sync.dma_start(out=out_v[:, T0[c] : T0[c] + nt, :], in_=o_r[c % 4][:, 0:nt, :])
 
         def w_perm(oh, copy):
-            src = w_sb[:, oh, :].rearrange("o (q c v h e j s) -> o c v h j q s e", q=16, c=2, v=2, h=2, e=2, j=NP, s=2)
-            for v in range(2):
+            src = w_sb[:, oh, :].rearrange("o (r h l e m s) -> o m h r e s l", r=4, h=2, l=2, e=16, m=NP, s=2)
+            for m in range(NP):
                 for h in range(2):
-                    for c in range(2):
-                        lo = 2 * (64 * v + 32 * c)
-                        copy(
-                            out=w_p[:, oh, :, h, lo : lo + 64].rearrange("o j (q s e) -> o j q s e", q=16, s=2, e=2),
-                            in_=src[:, c, v, h],
-                        )
+                    copy(
+                        out=w_p[:, oh, m, h, :].rearrange("o (r e s l) -> o r e s l", r=4, e=16, s=2, l=2),
+                        in_=src[:, m, h],
+                    )
 
         def w_trans():
             for m in range(NP):
@@ -241,21 +236,11 @@ def tile_cfkanlayer_kernel(tc, x, cheby_coeffs, bias, out):
                 scales=w_qs[:].rearrange("p m o -> p (m o)"),
                 in_=w_g[:].rearrange("p m f -> p (m f)").bitcast(BF16),
             )
-            for v in range(2):
-                for t in range(GP):
-                    rows, src = slice(64 * t, 64 * t + 64), slice(64 * v, 64 * v + 64)
-                    cols = slice(t * D_OUT, (t + 1) * D_OUT)
-                    nc.sync.dma_start(out=w_c[v][rows, :, cols].bitcast(I32), in_=w_q[src].bitcast(I32))
-                    nc.sync.dma_start(out=w_s[v][rows, :, cols].bitcast(I32), in_=w_qs[src].bitcast(I32))
 
         tanh(0)
         ttrans(0)
         tanh(1)
         nc.vector.memset(ones[:], 1.0)
-        nc.vector.memset(w_qs[:].bitcast(I32), 0)
-        for v in range(2):
-            nc.vector.memset(w_c[v][:].bitcast(I32), 0)
-            nc.vector.memset(w_s[v][:].bitcast(I32), 0)
         nc.sync.dma_start(out=sx[:, 0, :], in_=ones[:, 0:GE])
         nc.sync.dma_start(out=sy[:, 0, :], in_=ones[:, 0:GE])
         for b in range(2):

@@ -25,6 +25,7 @@ NCH = len(NG)
 T0 = [GP * sum(NG[:c]) for c in range(NCH)]
 FD = max(NG) * GE
 NP = KD // 2
+ALIGN = 256
 FLOPS = 2 * N_TOK * D_OUT * D_IN * KD
 
 
@@ -37,14 +38,15 @@ def tile_cfkanlayer_kernel(tc, x, cheby_coeffs, bias, out):
         ps = ctx.enter_context(tc.psum_pool(name="ps", bufs=1))
         ctx.enter_context(tc.manual_schedule())
 
-        def ring(n, shape, dtype, name, pool=keep, align=None):
-            if align is None:
-                return [pool.tile(shape, dtype, name="%s_%d" % (name, b)) for b in range(n)]
-            return [pool.tile(shape, dtype, name="%s_%d" % (name, b), align_bytes=align) for b in range(n)]
+        def ring(n, shape, dtype, name):
+            return [keep.tile(shape, dtype, name="%s_%d" % (name, b), align_bytes=ALIGN) for b in range(n)]
+
+        def banks(n, shape, name):
+            return [ps.tile(shape, F32, name="%s_%d" % (name, b)) for b in range(n)]
 
         x_r = ring(6, [P, 2 * GP, D_IN], BF16, "x")
-        w_sb = keep.tile([P, 2, D_IN * KD], BF16)
-        b_bf = keep.tile([P, D_OUT], BF16)
+        w_sb = keep.tile([P, 2, D_IN * KD], BF16, align_bytes=ALIGN)
+        b_bf = keep.tile([P, D_OUT], BF16, align_bytes=ALIGN)
 
         def x_load(c):
             n = GP * NG[c]
@@ -59,7 +61,7 @@ def tile_cfkanlayer_kernel(tc, x, cheby_coeffs, bias, out):
         x_load(3)
         nc.sync.dma_start(out=b_bf[:], in_=bias.rearrange("a o -> (a o)").partition_broadcast(P))
 
-        ident = keep.tile([P, P], F32)
+        ident = keep.tile([P, P], F32, align_bytes=ALIGN)
         make_identity(nc, ident[:])
 
         tn_r = ring(2, [P, 2, GE], F32, "tn")
@@ -70,23 +72,22 @@ def tile_cfkanlayer_kernel(tc, x, cheby_coeffs, bias, out):
         mm_r = ring(1, [P, FD], F32, "mm")
         pe_r = ring(3, [P, NP - 1, FD], BF16, "pe")
         p1_r = ring(3, [P, FD], BF16, "p1")
-        mx_r = ring(2, [P, NP, FD], BF16, "mx", align=64)
-        my_r = ring(2, [P, NP, FD], BF16, "my", align=64)
-        sx = keep.tile([P, NP, GE], BF16, align_bytes=64)
-        sy = keep.tile([P, NP, GE], BF16, align_bytes=64)
-        so = keep.tile([P, NP, GE], BF16)
-        cod_r = ring(2, [P, 2, NP, FD // 4], U32, "cod", align=64)
-        scl_r = ring(2, [P, 2, NP, FD // 4], U8, "scl", align=64)
+        mx_r = ring(2, [P, NP, FD], BF16, "mx")
+        my_r = ring(2, [P, NP, FD], BF16, "my")
+        sx = keep.tile([P, NP, GE], BF16, align_bytes=ALIGN)
+        sy = keep.tile([P, NP, GE], BF16, align_bytes=ALIGN)
+        so = keep.tile([P, NP, GE], BF16, align_bytes=ALIGN)
+        cod_r = ring(2, [P, 2, NP, FD // 4], U32, "cod")
+        scl_r = ring(2, [P, 2, NP, FD // 4], U8, "scl")
         o_r = ring(4, [P, 2 * GP, D_OUT], F32, "o")
-        tp_r = ring(4, [P, DP, P], F32, "tp", pool=ps)
-        acc_r = ring(4, [P, GP, D_OUT], F32, "acc", pool=ps)
-        ones = keep.tile([P, FD], BF16)
+        tp_r = banks(4, [P, DP, P], "tp")
+        acc_r = banks(4, [P, GP, D_OUT], "acc")
         trig = keep.tile([P, 1], F32)
         b_f32 = keep.tile([P, D_OUT], F32)
         w_p = keep.tile([P, 2, NP, 2, 2 * P], BF16)
-        w_g = keep.tile([P, NP, 2 * D_OUT], F32, align_bytes=64)
-        w_q = keep.tile([P, NP, D_OUT], U32, align_bytes=64)
-        w_qs = keep.tile([P, NP, D_OUT], U8, align_bytes=64)
+        w_g = keep.tile([P, NP, 2 * D_OUT], F32, align_bytes=ALIGN)
+        w_q = keep.tile([P, NP, D_OUT], U32, align_bytes=ALIGN)
+        w_qs = keep.tile([P, NP, D_OUT], U8, align_bytes=ALIGN)
 
         def ok(c):
             return 0 <= c < NCH
@@ -181,6 +182,11 @@ def tile_cfkanlayer_kernel(tc, x, cheby_coeffs, bias, out):
                 out=codes.bitcast(FP8X4), scales=scales, in_=mixed(c, v)[:].rearrange("p m f -> p (m f)")
             )
 
+        def sums(c, g, v):
+            if c == NCH - 1:
+                return acc_r[2 * (c % 2) + v][:, 0, :]
+            return acc_r[2 * (c % 2) + g][:, v, :]
+
         def mx(c):
             n = fd(c) // 4
             for v in range(2):
@@ -188,7 +194,7 @@ def tile_cfkanlayer_kernel(tc, x, cheby_coeffs, bias, out):
                     for m in range(NP):
                         cols = slice(m * n + g * P, m * n + (g + 1) * P)
                         nc.tensor.matmul_mx(
-                            out=acc_r[2 * (c % 2) + g][:, v, :],
+                            out=sums(c, g, v),
                             lhsT=cod_r[c % 2][:, v].rearrange("p m n -> p (m n)")[:, cols].bitcast(FP8X4),
                             lhsT_scale=scl_r[c % 2][:, v].rearrange("p m n -> p (m n)")[:, cols],
                             rhs=w_q[:, m, :].bitcast(FP8X4),
@@ -196,6 +202,12 @@ def tile_cfkanlayer_kernel(tc, x, cheby_coeffs, bias, out):
                             start=(m == 0),
                             stop=(m == NP - 1),
                         )
+
+        def last_out():
+            c = NCH - 1
+            for v in range(GP):
+                nc.vector.tensor_tensor(out=o_r[c % 4][:, v, :], in0=sums(c, 0, v), in1=b_f32[:], op=ALU.add)
+                nc.sync.dma_start(out=out_v[:, T0[c] + v, :], in_=o_r[c % 4][:, v, :])
 
         def outp(c):
             for g in groups(c):
@@ -205,6 +217,8 @@ def tile_cfkanlayer_kernel(tc, x, cheby_coeffs, bias, out):
                     in1=b_f32[:].unsqueeze(1).to_broadcast([P, GP, D_OUT]),
                     op=ALU.add,
                 )
+
+        def store(c):
             nt = GP * NG[c]
             nc.sync.dma_start(out=out_v[:, T0[c] : T0[c] + nt, :], in_=o_r[c % 4][:, 0:nt, :])
 
@@ -240,12 +254,35 @@ def tile_cfkanlayer_kernel(tc, x, cheby_coeffs, bias, out):
         tanh(0)
         ttrans(0)
         tanh(1)
-        nc.vector.memset(ones[:], 1.0)
-        nc.sync.dma_start(out=sx[:, 0, :], in_=ones[:, 0:GE])
-        nc.sync.dma_start(out=sy[:, 0, :], in_=ones[:, 0:GE])
-        for b in range(2):
-            nc.sync.dma_start(out=mx_r[b][:, 0, :], in_=ones[:])
-            nc.sync.dma_start(out=my_r[b][:, 0, :], in_=ones[:])
+        for tile in (sx, sy, mx_r[0], my_r[0]):
+            nc.vector.memset(tile[:, 0, :], 1.0)
+        for tile in (mx_r[1], my_r[1]):
+            nc.gpsimd.memset(tile[:, 0, :], 1.0)
+
+        def late(b):
+            stt(mm(b), v4(b), 2.0, t3(b))
+            if b >= NCH - 1:
+                act(odd(b, 1)[:, 0 : fd(b)], t3(b), ACTF.Identity)
+                act(even(b, 0, 2), zv_r[b % 3][:, :, 0 : fd(b)], ACTF.Identity, scale=0.5, bias_=-1.0)
+            else:
+                if b < 4:
+                    affine(nc.gpsimd, trig[:], mm(b)[:, fd(b) - 1 : fd(b)], 1.0, 0.0)
+                affine(nc.gpsimd, odd(b, 1)[:, 0 : fd(b)], t3(b), 1.0, 0.0)
+                affine(nc.gpsimd, even(b, 0, 2), zv_r[b % 3][:, :, 0 : fd(b)], 0.5, -1.0)
+                if b < 2:
+                    affine(nc.gpsimd, even(b, 2, 3)[:, 0, :], w6(b), 0.5, -1.0)
+            for g in groups(b):
+                stt(ni(odd(b, 2), g), ni(q5(b), g), 1.25, t_ps(b, g))
+            for g in groups(b):
+                nc.vector.tensor_tensor(out=ni(odd(b, 3), g), in0=ni(mm(b), g), in1=t_ps(b, g), op=ALU.subtract)
+            swap(b)
+            if b == 0 or b >= NCH - 2:
+                swap_rest(b)
+
+        def squares(b):
+            act(w6(b), t3(b), ACTF.Square, scale=2.0)
+            if b >= 2:
+                act(even(b, 2, 3)[:, 0, :], w6(b), ACTF.Identity, scale=0.5, bias_=-1.0)
 
         for i in range(NCH + 3):
             a, b, c, d, e = i, i - 1, i - 2, i - 3, i - 4
@@ -253,28 +290,8 @@ def tile_cfkanlayer_kernel(tc, x, cheby_coeffs, bias, out):
                 for g in groups(a):
                     act(ni(z(a), g), t_ps(a, g), ACTF.Square, scale=2.0)
             if ok(b):
-                act(w6(b), t3(b), ACTF.Square, scale=2.0)
-                if b >= 2:
-                    act(even(b, 2, 3)[:, 0, :], w6(b), ACTF.Identity, scale=0.5, bias_=-1.0)
-            if ok(b):
-                stt(mm(b), v4(b), 2.0, t3(b))
-                if b == NCH - 1:
-                    act(odd(b, 1), t3(b), ACTF.Identity)
-                    act(even(b, 0, 2), zv_r[b % 3][:, :, 0 : fd(b)], ACTF.Identity, scale=0.5, bias_=-1.0)
-                else:
-                    if b < 4:
-                        affine(nc.gpsimd, trig[:], mm(b)[:, fd(b) - 1 : fd(b)], 1.0, 0.0)
-                    affine(nc.gpsimd, odd(b, 1)[:, 0 : fd(b)], t3(b), 1.0, 0.0)
-                    affine(nc.gpsimd, even(b, 0, 2), zv_r[b % 3][:, :, 0 : fd(b)], 0.5, -1.0)
-                    if b < 2:
-                        affine(nc.gpsimd, even(b, 2, 3)[:, 0, :], w6(b), 0.5, -1.0)
-                for g in groups(b):
-                    stt(ni(odd(b, 2), g), ni(q5(b), g), 1.25, t_ps(b, g))
-                for g in groups(b):
-                    nc.vector.tensor_tensor(out=ni(odd(b, 3), g), in0=ni(mm(b), g), in1=t_ps(b, g), op=ALU.subtract)
-                swap(b)
-                if b == 0 or b >= NCH - 2:
-                    swap_rest(b)
+                squares(b)
+                late(b)
             if 0 < a and ok(a + 1):
                 tanh(a + 1)
             if ok(a):
@@ -298,15 +315,24 @@ def tile_cfkanlayer_kernel(tc, x, cheby_coeffs, bias, out):
                 w_trans()
             if ok(a + 4):
                 x_load(a + 4)
+            if i == NCH:
+                for k in range(NCH - 5, NCH - 4):
+                    store(k)
             if 0 <= e < NCH - 3:
                 outp(e)
+                if not NCH - 6 < e < NCH - 4:
+                    store(e)
             if ok(c):
                 for v in range(2):
                     quant(c, v)
             if d == NCH - 3:
                 outp(e + 1)
-            if ok(d) and c >= NCH - 1:
+                store(e + 1)
+            if d == NCH - 2:
                 outp(d)
+                store(d)
+            if d == NCH - 1:
+                last_out()
             if 0 < b < NCH - 2:
                 swap_rest(b)
             if ok(c):

from contextlib import ExitStack

import concourse.mybir as mybir
from concourse.masks import make_identity

F32 = mybir.dt.float32
BF16 = mybir.dt.bfloat16
U32 = mybir.dt.uint32
U8 = mybir.dt.uint8
FP8X4 = mybir.dt.float8_e4m3fn_x4
ALU = mybir.AluOpType
ACTF = mybir.ActivationFunctionType

P = 128
N_TOK = 8192
D_IN = 256
KD = 8
D_OUT = 256
NT = N_TOK // P
GP = 2
DP = 4
GE = DP * P
NG = (1,) + (2,) * 15 + (1,)
NCH = len(NG)
T0 = [GP * sum(NG[:c]) for c in range(NCH)]
FD = max(NG) * GE
NP = KD // 2
ALIGN = 256
FLOPS = 2 * N_TOK * D_OUT * D_IN * KD


def tile_cfkanlayer_kernel(tc, x, cheby_coeffs, bias, out):
    nc = tc.nc
    x_v = x.rearrange("(p t) d -> p t d", t=NT)
    out_v = out.rearrange("(p t) o -> p t o", t=NT)
    with ExitStack() as ctx:
        keep = ctx.enter_context(tc.tile_pool(name="keep", bufs=1))
        ps = ctx.enter_context(tc.psum_pool(name="ps", bufs=1))
        ctx.enter_context(tc.manual_schedule())

        def ring(n, shape, dtype, name):
            return [keep.tile(shape, dtype, name="%s_%d" % (name, b), align_bytes=ALIGN) for b in range(n)]

        def banks(n, shape, name):
            return [ps.tile(shape, F32, name="%s_%d" % (name, b)) for b in range(n)]

        x_r = ring(6, [P, 2 * GP, D_IN], BF16, "x")
        w_sb = keep.tile([P, 2, D_IN * KD], BF16, align_bytes=ALIGN)
        b_bf = keep.tile([P, D_OUT], BF16, align_bytes=ALIGN)

        def x_load(c):
            n = GP * NG[c]
            nc.sync.dma_start(out=x_r[c % 6][:, 0:n, :], in_=x_v[:, T0[c] : T0[c] + n, :])

        x_load(0)
        x_load(1)
        w_v = cheby_coeffs.rearrange("(h o) d k -> o h (d k)", h=2)
        for oh in range(2):
            nc.sync.dma_start(out=w_sb[:, oh, :], in_=w_v[:, oh, :])
        x_load(2)
        x_load(3)
        nc.sync.dma_start(out=b_bf[:], in_=bias.rearrange("a o -> (a o)").partition_broadcast(P))

        ident = keep.tile([P, P], F32, align_bytes=ALIGN)
        make_identity(nc, ident[:])

        tn_r = ring(2, [P, 2, GE], F32, "tn")
        zv_r = ring(3, [P, 2, FD], F32, "zv")
        w6_r = ring(2, [P, FD], F32, "w6")
        q5_r = ring(3, [P, FD], F32, "q5")
        t3_r = ring(2, [P, FD], F32, "t3")
        mm_r = ring(1, [P, FD], F32, "mm")
        pe_r = ring(3, [P, NP - 1, FD], BF16, "pe")
        p1_r = ring(3, [P, FD], BF16, "p1")
        mx_r = ring(2, [P, NP, FD], BF16, "mx")
        my_r = ring(2, [P, NP, FD], BF16, "my")
        sx = keep.tile([P, NP, GE], BF16, align_bytes=ALIGN)
        sy = keep.tile([P, NP, GE], BF16, align_bytes=ALIGN)
        so = keep.tile([P, NP, GE], BF16, align_bytes=ALIGN)
        cod_r = ring(2, [P, 2, NP, FD // 4], U32, "cod")
        scl_r = ring(2, [P, 2, NP, FD // 4], U8, "scl")
        o_r = ring(4, [P, 2 * GP, D_OUT], F32, "o")
        tp_r = banks(4, [P, DP, P], "tp")
        acc_r = banks(4, [P, GP, D_OUT], "acc")
        trig = keep.tile([P, 1], F32)
        b_f32 = keep.tile([P, D_OUT], F32)
        w_p = keep.tile([P, 2, NP, 2, 2 * P], BF16)
        w_g = keep.tile([P, NP, 2 * D_OUT], F32, align_bytes=ALIGN)
        w_q = keep.tile([P, NP, D_OUT], U32, align_bytes=ALIGN)
        w_qs = keep.tile([P, NP, D_OUT], U8, align_bytes=ALIGN)

        def ok(c):
            return 0 <= c < NCH

        def groups(c):
            return range(NG[c])

        def fd(c):
            return NG[c] * GE

        def ni(ap, g):
            return ap[:, g * GE : (g + 1) * GE].rearrange("p (n i) -> p n i", i=DP)

        def t_ps(c, g):
            return tp_r[2 * (c % 2) + g][:].rearrange("p i n -> p n i")

        def z(c):
            return zv_r[c % 3][:, 0, 0 : fd(c)]

        def v4(c):
            return zv_r[c % 3][:, 1, 0 : fd(c)]

        def q5(c):
            return q5_r[c % 3][:, 0 : fd(c)]

        def t3(c):
            return t3_r[c % 2][:, 0 : fd(c)]

        def w6(c):
            return w6_r[c % 2][:, 0 : fd(c)]

        def mm(c):
            return mm_r[0][:, 0 : fd(c)]

        def even(c, lo, hi):
            return pe_r[c % 3][:, lo:hi, 0 : fd(c)]

        def mixed(c, v):
            if NG[c] == 1:
                return (sx, sy)[v]
            return (mx_r, my_r)[v][c % 2]

        def odds(c):
            return so if NG[c] == 1 else mixed(c, 1)

        def odd(c, m):
            return odds(c)[:, m, :]

        def act(o, i, f, scale=1.0, bias_=0.0):
            nc.scalar.activation(out=o, in_=i, func=f, scale=scale, bias=bias_)

        def tanh(c):
            for tl in range(GP * NG[c]):
                act(
                    tn_r[c % 2][:, tl // GP, :].rearrange("p (r e t j) -> p t r e j", r=4, e=16, t=GP)[:, tl % GP],
                    x_r[c % 6][:, tl, :].rearrange("p (r j e) -> p r e j", r=4, j=DP),
                    ACTF.Tanh,
                )

        def ttrans(c):
            for g in groups(c):
                words = tn_r[c % 2][:, g, :]
                for i in range(DP):
                    nc.tensor.transpose(tp_r[2 * (c % 2) + g][:, i, :], words[:, i : GE : DP], ident[:])

        def stt(o, a, s, b):
            nc.vector.scalar_tensor_tensor(out=o, in0=a, scalar=s, in1=b, op0=ALU.subtract, op1=ALU.mult)

        def affine(eng, o, i, s, b):
            eng.tensor_scalar(out=o, in0=i, scalar1=s, scalar2=b, op0=ALU.mult, op1=ALU.add)

        def t1(c):
            return p1_r[c % 3][:, 0 : fd(c)]

        def swap(c):
            xm, ym = mixed(c, 0), mixed(c, 1)
            nc.sync.dma_start(out=xm[1:P:2, 0, :], in_=t1(c)[0:P:2])
            nc.sync.dma_start(out=ym[1:P:2, 0, :], in_=t1(c)[1:P:2])
            nc.sync.dma_start(out=xm[1:P:2, 1:NP, :], in_=odds(c)[0:P:2, 1:NP, :])
            if NG[c] == 1:
                nc.sync.dma_start(out=ym[1:P:2, 1:NP, :], in_=so[1:P:2, 1:NP, :])
            nc.sync.dma_start(out=xm[0:P:2, 1:NP, :], in_=even(c, 0, NP - 1)[0:P:2])

        def swap_rest(c):
            nc.sync.dma_start(out=mixed(c, 1)[0:P:2, 1:NP, :], in_=even(c, 0, NP - 1)[1:P:2])

        def quant(c, v):
            n = fd(c) // 4
            codes = cod_r[c % 2][:, v].rearrange("p m n -> p (m n)")[:, 0 : NP * n]
            scales = scl_r[c % 2][:, v].rearrange("p m n -> p (m n)")[:, 0 : NP * n]
            nc.vector.quantize_mx(
                out=codes.bitcast(FP8X4), scales=scales, in_=mixed(c, v)[:].rearrange("p m f -> p (m f)")
            )

        def sums(c, g, v):
            if c == NCH - 1:
                return acc_r[2 * (c % 2) + v][:, 0, :]
            return acc_r[2 * (c % 2) + g][:, v, :]

        def mx(c):
            n = fd(c) // 4
            for v in range(2):
                for g in groups(c):
                    for m in range(NP):
                        cols = slice(m * n + g * P, m * n + (g + 1) * P)
                        nc.tensor.matmul_mx(
                            out=sums(c, g, v),
                            lhsT=cod_r[c % 2][:, v].rearrange("p m n -> p (m n)")[:, cols].bitcast(FP8X4),
                            lhsT_scale=scl_r[c % 2][:, v].rearrange("p m n -> p (m n)")[:, cols],
                            rhs=w_q[:, m, :].bitcast(FP8X4),
                            rhs_scale=w_qs[:, m, :],
                            start=(m == 0),
                            stop=(m == NP - 1),
                        )

        def last_out():
            c = NCH - 1
            for v in range(GP):
                nc.vector.tensor_tensor(out=o_r[c % 4][:, v, :], in0=sums(c, 0, v), in1=b_f32[:], op=ALU.add)
                nc.sync.dma_start(out=out_v[:, T0[c] + v, :], in_=o_r[c % 4][:, v, :])

        def outp(c):
            for g in groups(c):
                nc.vector.tensor_tensor(
                    out=o_r[c % 4][:, GP * g : GP * (g + 1), :],
                    in0=acc_r[2 * (c % 2) + g][:],
                    in1=b_f32[:].unsqueeze(1).to_broadcast([P, GP, D_OUT]),
                    op=ALU.add,
                )

        def store(c):
            nt = GP * NG[c]
            nc.sync.dma_start(out=out_v[:, T0[c] : T0[c] + nt, :], in_=o_r[c % 4][:, 0:nt, :])

        def w_perm(oh, copy):
            src = w_sb[:, oh, :].rearrange("o (r h l e m s) -> o m h r e s l", r=4, h=2, l=2, e=16, m=NP, s=2)
            for m in range(NP):
                for h in range(2):
                    copy(
                        out=w_p[:, oh, m, h, :].rearrange("o (r e s l) -> o r e s l", r=4, e=16, s=2, l=2),
                        in_=src[:, m, h],
                    )

        def w_trans():
            for m in range(NP):
                for h in range(2):
                    for oh in range(2):
                        nc.tensor.transpose(
                            acc_r[m][:, h, oh * P : (oh + 1) * P], w_p[:, oh, m, h, :].bitcast(F32), ident[:]
                        )

        def w_copy(m):
            nc.vector.tensor_copy(
                out=w_g[:, m, :].rearrange("p (o h) -> p o h", h=2), in_=acc_r[m][:].rearrange("p h o -> p o h")
            )

        def w_quant():
            nc.vector.quantize_mx(
                out=w_q[:].rearrange("p m o -> p (m o)").bitcast(FP8X4),
                scales=w_qs[:].rearrange("p m o -> p (m o)"),
                in_=w_g[:].rearrange("p m f -> p (m f)").bitcast(BF16),
            )

        tanh(0)
        ttrans(0)
        tanh(1)
        for tile in (sx, sy, mx_r[0], my_r[0]):
            nc.vector.memset(tile[:, 0, :], 1.0)
        for tile in (mx_r[1], my_r[1]):
            nc.gpsimd.memset(tile[:, 0, :], 1.0)

        def late(b):
            stt(mm(b), v4(b), 2.0, t3(b))
            if b >= NCH - 1:
                act(odd(b, 1)[:, 0 : fd(b)], t3(b), ACTF.Identity)
                act(even(b, 0, 2), zv_r[b % 3][:, :, 0 : fd(b)], ACTF.Identity, scale=0.5, bias_=-1.0)
            else:
                if b < 4:
                    affine(nc.gpsimd, trig[:], mm(b)[:, fd(b) - 1 : fd(b)], 1.0, 0.0)
                affine(nc.gpsimd, odd(b, 1)[:, 0 : fd(b)], t3(b), 1.0, 0.0)
                affine(nc.gpsimd, even(b, 0, 2), zv_r[b % 3][:, :, 0 : fd(b)], 0.5, -1.0)
                if b < 2:
                    affine(nc.gpsimd, even(b, 2, 3)[:, 0, :], w6(b), 0.5, -1.0)
            for g in groups(b):
                stt(ni(odd(b, 2), g), ni(q5(b), g), 1.25, t_ps(b, g))
            for g in groups(b):
                nc.vector.tensor_tensor(out=ni(odd(b, 3), g), in0=ni(mm(b), g), in1=t_ps(b, g), op=ALU.subtract)
            swap(b)
            if b == 0 or b >= NCH - 2:
                swap_rest(b)

        def squares(b):
            act(w6(b), t3(b), ACTF.Square, scale=2.0)
            if b >= 2:
                act(even(b, 2, 3)[:, 0, :], w6(b), ACTF.Identity, scale=0.5, bias_=-1.0)

        for i in range(NCH + 3):
            a, b, c, d, e = i, i - 1, i - 2, i - 3, i - 4
            if ok(a):
                for g in groups(a):
                    act(ni(z(a), g), t_ps(a, g), ACTF.Square, scale=2.0)
            if ok(b):
                squares(b)
                late(b)
            if 0 < a and ok(a + 1):
                tanh(a + 1)
            if ok(a):
                for g in groups(a):
                    stt(ni(t3(a), g), ni(z(a), g), 3.0, t_ps(a, g))
                act(v4(a), z(a), ACTF.Square, bias_=-2.0)
                act(q5(a), z(a), ACTF.Square, bias_=-2.5)
                for g in groups(a):
                    nc.scalar.copy(out=ni(t1(a), g), in_=t_ps(a, g))
            if i == 0:
                w_perm(0, nc.vector.tensor_copy)
                w_perm(1, nc.scalar.copy)
            if i == 1:
                affine(nc.gpsimd, b_f32[:], b_bf[:], 1.0, 0.0)
                for m in range(NP):
                    w_copy(m)
                w_quant()
            if ok(a + 1):
                ttrans(a + 1)
            if i == 0:
                w_trans()
            if ok(a + 4):
                x_load(a + 4)
            if i == NCH:
                for k in range(NCH - 5, NCH - 4):
                    store(k)
            if 0 <= e < NCH - 3:
                outp(e)
                if not NCH - 6 < e < NCH - 4:
                    store(e)
            if ok(c):
                for v in range(2):
                    quant(c, v)
            if d == NCH - 3:
                outp(e + 1)
                store(e + 1)
            if d == NCH - 2:
                outp(d)
                store(d)
            if d == NCH - 1:
                last_out()
            if 0 < b < NCH - 2:
                swap_rest(b)
            if ok(c):
                mx(c)
